import numpy as np
import ml_dtypes


def mxq(x, axis, fmt="e4m3"):
    dtype, down = {"e4m3": (ml_dtypes.float8_e4m3fn, 7), "e5m2": (ml_dtypes.float8_e5m2, 14)}[fmt]
    v = np.moveaxis(np.asarray(x, np.float32).astype(ml_dtypes.bfloat16).astype(np.float64), axis, -1)
    blocks = v.reshape(v.shape[:-1] + (-1, 32))
    amax = np.abs(blocks).max(-1, keepdims=True)
    byte = np.maximum(np.where(amax > 0, np.frexp(amax)[1] - 1 + 127, 0) - down, 1)
    scale = np.exp2(byte - 127.0)
    codes = (blocks / scale).astype(np.float32).astype(dtype).astype(np.float64)
    return np.moveaxis((codes * scale).reshape(v.shape), -1, axis)


WIDE = False


def mx_kscale(k):
    if not WIDE:
        return np.ones(k)
    levels = np.array([10, -10, 5, -5, 0])
    a = np.random.permutation(np.resize(levels, k // 512 * 4)).reshape(k // 512, 4)
    idx = np.arange(k)
    return np.exp2(a[idx // 512, idx % 128 // 32])


BF16 = ml_dtypes.bfloat16


def bf(x):
    return np.asarray(x, np.float32).astype(BF16)


def f64(x):
    return np.asarray(x).astype(np.float64)


E2M1 = np.array([0.0, 0.5, 1.0, 1.5, 2.0, 3.0, 4.0, 6.0, -0.0, -0.5, -1.0, -1.5, -2.0, -3.0, -4.0, -6.0])


def pack_weight(w, fmt):
    k, n = w.shape
    w = f64(bf(w)).reshape(k // 32, 32, n)
    amax = np.abs(w).max(1)
    if fmt == "e4m3":
        byte = np.frexp(amax)[1] - 1 + 127 - 7
    else:
        mant, ex = np.frexp(amax / 6.0)
        byte = np.where(mant > 0.5, ex, ex - 1) + 127
    byte = np.clip(np.where(amax > 0, byte, 1), 1, 254)
    scaled = (w * np.exp2(127.0 - byte)[:, None, :]).reshape(k, n).astype(np.float32)
    by_word = np.ascontiguousarray(scaled.reshape(k // 512, 128, 4, n).transpose(0, 1, 3, 2))
    if fmt == "e4m3":
        words = by_word.astype(ml_dtypes.float8_e4m3fn).view(np.uint8)
    else:
        c = by_word.astype(ml_dtypes.float4_e2m1fn).view(np.uint8) & 0xF
        words = c[..., 0::2] | (c[..., 1::2] << 4)
    return np.ascontiguousarray(words), np.ascontiguousarray(byte.astype(np.uint8).reshape(k // 512, 16, n))


def unpack_weight(words, scales, fmt):
    g, p, n, _ = words.shape
    if fmt == "e4m3":
        vals = np.ascontiguousarray(words).view(ml_dtypes.float8_e4m3fn).astype(np.float64)
    else:
        nib = np.empty((g, p, n, 4), np.uint8)
        nib[..., 0::2] = words & 0xF
        nib[..., 1::2] = words >> 4
        vals = E2M1[nib]
    vals = vals * np.repeat(np.exp2(scales.astype(np.float64) - 127.0), 8, axis=1)[..., None]
    return vals.transpose(0, 1, 3, 2).reshape(g * 512, n)

def pack4(w):
    words, scales = pack_weight(w, "e2m1")
    return words.reshape(words.shape[0], 128, -1), scales


def unpack4(words, scales):
    return unpack_weight(words.reshape(words.shape[0], 128, -1, 2), scales, "e2m1")


B, D, H = 4096, 512, 512
M_SCALE = 1.5


def setup_inputs():
    s, t = mx_kscale(D), mx_kscale(H)
    x = bf(np.random.standard_normal((B, D)) * s)
    h_prev = bf(np.random.standard_normal((B, H)) * t)
    c_prev = bf(np.random.standard_normal((B, H)))
    W_ih = np.random.standard_normal((2 * H, D)) * 0.7 / np.sqrt(D) / s[None, :]
    b_ih = bf(np.random.standard_normal(2 * H) * 0.2)
    W_hh = np.random.standard_normal((2 * H, H)) * 0.7 / np.sqrt(H) / t[None, :]
    b_hh = bf(np.random.standard_normal(2 * H) * 0.2)
    log_lambda = bf(np.log(np.random.uniform(0.05, 0.5, H)))
    z_bias = bf(np.random.standard_normal(H) * 0.2)
    m_bias = bf(np.random.standard_normal(H) * 0.2)
    W_ih_words, W_ih_scales = pack4(np.ascontiguousarray(W_ih.T))
    W_hh_words, W_hh_scales = pack4(np.ascontiguousarray(W_hh.T))
    return {'x': x,
            'h_prev': h_prev,
            'c_prev': c_prev,
            'W_ih_words': W_ih_words,
            'W_ih_scales': W_ih_scales,
            'b_ih': b_ih,
            'W_hh_words': W_hh_words,
            'W_hh_scales': W_hh_scales,
            'b_hh': b_hh,
            'log_lambda': log_lambda,
            'z_bias': z_bias,
            'm_bias': m_bias}


def reference(x, h_prev, c_prev, W_ih_words, W_ih_scales, b_ih, W_hh_words, W_hh_scales, b_hh, log_lambda, z_bias, m_bias):
    gates = ((mxq(f64(x), 1, 'e4m3') @ unpack4(W_ih_words, W_ih_scales)) + f64(b_ih)
             + (mxq(f64(h_prev), 1, 'e4m3') @ unpack4(W_hh_words, W_hh_scales)) + f64(b_hh))
    z_raw, m_raw = gates[:, :H], gates[:, H:]
    z_t = np.tanh(z_raw + f64(z_bias))
    M_t = M_SCALE * np.tanh(m_raw + f64(m_bias))
    A_base = -np.exp(f64(log_lambda))
    innov = z_t - M_t * (A_base * f64(c_prev))
    return z_t, M_t, innov

@@ -1,0 +1,248 @@
+from contextlib import ExitStack
+
+import concourse.mybir as mybir
+from concourse.masks import make_identity
+
+F32 = mybir.dt.float32
+BF16 = mybir.dt.bfloat16
+I32 = mybir.dt.int32
+U32 = mybir.dt.uint32
+U8 = mybir.dt.uint8
+FP8X4 = mybir.dt.float8_e4m3fn_x4
+FP4X4 = mybir.dt.float4_e2m1fn_x4
+ADD = mybir.AluOpType.add
+MULT = mybir.AluOpType.mult
+ACT = mybir.ActivationFunctionType
+
+P = 128
+BATCH = 4096
+K = 512
+H = 512
+M_SCALE = 1.5
+TILES = BATCH // P
+CHUNK = 4
+CHUNKS = TILES // CHUNK
+AHEAD = 2
+
+FLOPS = 2 * BATCH * (2 * K) * (2 * H)
+
+
+def tile_koslmcell_pa_t_kernel(
+    tc,
+    x,
+    h_prev,
+    c_prev,
+    W_ih_words,
+    W_ih_scales,
+    b_ih,
+    W_hh_words,
+    W_hh_scales,
+    b_hh,
+    log_lambda,
+    z_bias,
+    m_bias,
+    out_0,
+    out_1,
+    out_2,
+):
+    nc = tc.nc
+
+    x_v = x.rearrange("(p t) k -> p t k", t=TILES)
+    h_v = h_prev.rearrange("(p t) k -> p t k", t=TILES)
+    c_v = c_prev.rearrange("(p t) k -> p t k", t=TILES)
+    z_v = out_0.rearrange("(p t) k -> p t k", t=TILES)
+    m_v = out_1.rearrange("(p t) k -> p t k", t=TILES)
+    i_v = out_2.rearrange("(p t) k -> p t k", t=TILES)
+
+    with ExitStack() as ctx:
+        const = ctx.enter_context(tc.tile_pool(name="const", bufs=1))
+        loads = ctx.enter_context(tc.tile_pool(name="loads", bufs=AHEAD + 1))
+        front = ctx.enter_context(tc.tile_pool(name="front", bufs=3))
+        middle = ctx.enter_context(tc.tile_pool(name="middle", bufs=3))
+        stores = ctx.enter_context(tc.tile_pool(name="stores", bufs=3))
+        psum_tr = ctx.enter_context(tc.psum_pool(name="psum_tr", bufs=2))
+        psum_acc = ctx.enter_context(tc.psum_pool(name="psum_acc", bufs=3))
+
+        live = {}
+
+        def load_chunk(c):
+            rows = slice(c * CHUNK, (c + 1) * CHUNK)
+            x_sb = loads.tile([P, CHUNK, K], BF16)
+            nc.sync.dma_start(out=x_sb[:], in_=x_v[:, rows, :])
+            h_sb = loads.tile([P, CHUNK, K], BF16)
+            nc.sync.dma_start(out=h_sb[:], in_=h_v[:, rows, :])
+            live["x", c] = x_sb
+            live["h", c] = h_sb
+
+        def load_cell(c):
+            rows = slice(c * CHUNK, (c + 1) * CHUNK)
+            c_sb = loads.tile([P, CHUNK, H], BF16)
+            nc.sync.dma_start(out=c_sb[:], in_=c_v[:, rows, :])
+            live["c", c] = c_sb
+
+        load_chunk(0)
+
+        ident = const.tile([P, P], F32)
+        make_identity(nc, ident[:])
+
+        words = {}
+        planes = {}
+        for name, w_words, w_scales in (("x", W_ih_words, W_ih_scales), ("h", W_hh_words, W_hh_scales)):
+            w_sb = const.tile([P, 4 * H], U8, name="words_" + name, align_bytes=64)
+            nc.sync.dma_start(out=w_sb[:].bitcast(I32), in_=w_words[0].bitcast(I32))
+            plane = const.tile([P, 2 * H], U8, name="plane_" + name, align_bytes=64)
+            nc.vector.memset(plane[:].bitcast(I32), 0)
+            for quad in range(4):
+                nc.sync.dma_start(
+                    out=plane[32 * quad : 32 * quad + 4, :].bitcast(I32),
+                    in_=w_scales[0, 4 * quad : 4 * quad + 4, :].bitcast(I32),
+                )
+            words[name] = w_sb
+            planes[name] = plane
+
+        ones = const.tile([P, P], BF16)
+        nc.vector.memset(ones[:], 1.0)
+        bias_rows = const.tile([P, 2 * H], BF16)
+        nc.vector.memset(bias_rows[:].bitcast(I32), 0)
+        lam_rows = const.tile([P, H], BF16)
+        nc.vector.memset(lam_rows[:].bitcast(I32), 0)
+        nc.sync.dma_start(out=bias_rows[0:1, :], in_=b_ih.rearrange("(o n) -> o n", o=1))
+        nc.sync.dma_start(out=bias_rows[1:2, :], in_=b_hh.rearrange("(o n) -> o n", o=1))
+        nc.sync.dma_start(out=bias_rows[2:3, 0:H], in_=z_bias.rearrange("(o n) -> o n", o=1))
+        nc.sync.dma_start(out=bias_rows[2:3, H : 2 * H], in_=m_bias.rearrange("(o n) -> o n", o=1))
+        nc.sync.dma_start(out=lam_rows[0:1, :], in_=log_lambda.rearrange("(o n) -> o n", o=1))
+
+        load_cell(0)
+        for c in range(1, AHEAD):
+            load_chunk(c)
+            load_cell(c)
+
+        bias_bc = const.tile([P, 2 * H], F32)
+        for g in range(2):
+            cols = slice(g * H, (g + 1) * H)
+            spread = psum_acc.tile([P, H], F32, tag="acc_z")
+            nc.tensor.matmul(out=spread[:], lhsT=ones[:], rhs=bias_rows[:, cols], start=True, stop=True)
+            nc.vector.tensor_copy(out=bias_bc[:, cols], in_=spread[:])
+        lam_bc = psum_acc.tile([P, H], F32, tag="acc_m")
+        nc.tensor.matmul(out=lam_bc[:], lhsT=ones[:], rhs=lam_rows[:], start=True, stop=True)
+        decay = const.tile([P, H], F32)
+        nc.scalar.activation(out=decay[:], in_=lam_bc[:], func=ACT.Exp)
+        decay_m = const.tile([P, H], F32)
+        nc.scalar.mul(decay_m[:], decay[:], M_SCALE)
+
+        def transpose_tile(i):
+            c, r = divmod(i, CHUNK)
+            turned = psum_tr.tile([P, 2, 2, P], F32)
+            for a, name in enumerate(("x", "h")):
+                as_words = live[name, c][:, r, :].bitcast(F32)
+                for u in range(2):
+                    nc.tensor.transpose(turned[:, a, u, :], as_words[:, u : K // 2 : 2], ident[:])
+            live["turned", i] = turned
+
+        def regroup_tile(i):
+            grouped = front.tile([P, 2, P, 4], BF16, align_bytes=64)
+            nc.scalar.copy(
+                out=grouped[:].bitcast(F32),
+                in_=live["turned", i][:].rearrange("p a u r -> p a r u"),
+            )
+            live["grouped", i] = grouped
+
+        def quantise_tile(i):
+            codes = front.tile([P, 2, P], U32, align_bytes=64)
+            scales = front.tile([P, 2, P], U8, align_bytes=64)
+            nc.vector.quantize_mx(
+                out=codes[:].rearrange("p a r -> p (a r)").bitcast(FP8X4),
+                scales=scales[:].rearrange("p a r -> p (a r)"),
+                in_=live["grouped", i][:].rearrange("p a r t -> p (a r t)"),
+            )
+            live["codes", i] = codes
+            live["scales", i] = scales
+
+        def multiply_tile(i):
+            acc_z = psum_acc.tile([P, H], F32)
+            acc_m = psum_acc.tile([P, H], F32)
+            for g, acc in enumerate((acc_z, acc_m)):
+                for a, name in enumerate(("x", "h")):
+                    nc.tensor.matmul_mx(
+                        out=acc[:],
+                        lhsT=live["codes", i][:, a, :].bitcast(FP8X4),
+                        lhsT_scale=live["scales", i][:, a, :],
+                        rhs=words[name][:, 2 * g * H : 2 * (g + 1) * H].bitcast(FP4X4),
+                        rhs_scale=planes[name][:, g * H : (g + 1) * H],
+                        start=(a == 0),
+                        stop=(a == 1),
+                    )
+            live["acc_z", i] = acc_z
+            live["acc_m", i] = acc_m
+
+        def add_bias_tile(i):
+            pre = middle.tile([P, 2 * H], F32)
+            nc.vector.tensor_tensor(out=pre[:, 0:H], in0=live["acc_z", i][:], in1=bias_bc[:, 0:H], op=ADD)
+            nc.vector.tensor_tensor(out=pre[:, H : 2 * H], in0=live["acc_m", i][:], in1=bias_bc[:, H : 2 * H], op=ADD)
+            live["pre", i] = pre
+
+        def squash_tile(i):
+            c, r = divmod(i, CHUNK)
+            if r == 0:
+                z_st = stores.tile([P, CHUNK, H], F32)
+                m_st = stores.tile([P, CHUNK, H], F32)
+                live["z", c] = z_st
+                live["m", c] = m_st
+            tanh_m = middle.tile([P, H], F32)
+            nc.scalar.activation(out=tanh_m[:], in_=live["pre", i][:, H : 2 * H], func=ACT.Tanh)
+            nc.scalar.activation(out=live["z", c][:, r, :], in_=live["pre", i][:, 0:H], func=ACT.Tanh)
+            nc.scalar.mul(live["m", c][:, r, :], tanh_m[:], M_SCALE)
+            live["tanh_m", i] = tanh_m
+
+        def scale_cell(c):
+            damped = middle.tile([P, CHUNK, H], F32)
+            nc.gpsimd.tensor_tensor(
+                out=damped[:],
+                in0=live["c", c][:],
+                in1=decay_m[:].unsqueeze(1).to_broadcast([P, CHUNK, H]),
+                op=MULT,
+            )
+            live["damped", c] = damped
+
+        def product_tile(i):
+            c, r = divmod(i, CHUNK)
+            if r == 0:
+                i_st = stores.tile([P, CHUNK, H], F32)
+                live["i", c] = i_st
+            nc.vector.tensor_tensor(
+                out=live["i", c][:, r, :], in0=live["tanh_m", i][:], in1=live["damped", c][:, r, :], op=MULT
+            )
+
+        def sum_tile(i):
+            c, r = divmod(i, CHUNK)
+            nc.vector.tensor_tensor(
+                out=live["i", c][:, r, :], in0=live["i", c][:, r, :], in1=live["z", c][:, r, :], op=ADD
+            )
+            if r == CHUNK - 1:
+                rows = slice(c * CHUNK, (c + 1) * CHUNK)
+                nc.sync.dma_start(out=z_v[:, rows, :], in_=live["z", c][:])
+                nc.sync.dma_start(out=m_v[:, rows, :], in_=live["m", c][:])
+                nc.sync.dma_start(out=i_v[:, rows, :], in_=live["i", c][:])
+
+        for j in range(TILES + 4):
+            if j < TILES and j % CHUNK == 0:
+                c = j // CHUNK
+                if c + AHEAD < CHUNKS:
+                    load_chunk(c + AHEAD)
+                    load_cell(c + AHEAD)
+                scale_cell(c)
+            if j < TILES:
+                transpose_tile(j)
+            if 0 <= j - 4 < TILES:
+                product_tile(j - 4)
+            if 0 <= j - 1 < TILES:
+                quantise_tile(j - 1)
+                multiply_tile(j - 1)
+            if 0 <= j - 4 < TILES:
+                sum_tile(j - 4)
+            if 0 <= j - 2 < TILES:
+                add_bias_tile(j - 2)
+            if 0 <= j - 3 < TILES:
+                squash_tile(j - 3)
+            if j < TILES:
+                regroup_tile(j)

@@ -21,8 +21,10 @@ H = 512
 M_SCALE = 1.5
 TILES = BATCH // P
 CHUNK = 4
+ROWS = CHUNK * P
 CHUNKS = TILES // CHUNK
-AHEAD = 2
+BLOCKS = H // P
+AHEAD = 3
 
 FLOPS = 2 * BATCH * (2 * K) * (2 * H)
 
@@ -54,14 +56,18 @@ def tile_koslmcell_pa_t_kernel(
     m_v = out_1.rearrange("(p t) k -> p t k", t=TILES)
     i_v = out_2.rearrange("(p t) k -> p t k", t=TILES)
 
+    def as_row(vector):
+        return vector.rearrange("(o n) -> o n", o=1)
+
+    def as_blocks(vector):
+        return vector.rearrange("(j p) -> j p", p=P)
+
     with ExitStack() as ctx:
         const = ctx.enter_context(tc.tile_pool(name="const", bufs=1))
         loads = ctx.enter_context(tc.tile_pool(name="loads", bufs=AHEAD + 1))
-        front = ctx.enter_context(tc.tile_pool(name="front", bufs=3))
-        middle = ctx.enter_context(tc.tile_pool(name="middle", bufs=3))
+        work = ctx.enter_context(tc.tile_pool(name="work", bufs=2))
         stores = ctx.enter_context(tc.tile_pool(name="stores", bufs=3))
-        psum_tr = ctx.enter_context(tc.psum_pool(name="psum_tr", bufs=2))
-        psum_acc = ctx.enter_context(tc.psum_pool(name="psum_acc", bufs=3))
+        psum = ctx.enter_context(tc.psum_pool(name="psum", bufs=2))
 
         live = {}
 
@@ -84,6 +90,8 @@ def tile_koslmcell_pa_t_kernel(
 
         ident = const.tile([P, P], F32)
         make_identity(nc, ident[:])
+        ident_bf = const.tile([P, P], BF16)
+        make_identity(nc, ident_bf[:])
 
         words = {}
         planes = {}
@@ -102,147 +110,142 @@ def tile_koslmcell_pa_t_kernel(
 
         ones = const.tile([P, P], BF16)
         nc.vector.memset(ones[:], 1.0)
-        bias_rows = const.tile([P, 2 * H], BF16)
-        nc.vector.memset(bias_rows[:].bitcast(I32), 0)
+        z_rows = const.tile([P, H], BF16)
+        nc.vector.memset(z_rows[:].bitcast(I32), 0)
         lam_rows = const.tile([P, H], BF16)
         nc.vector.memset(lam_rows[:].bitcast(I32), 0)
-        nc.sync.dma_start(out=bias_rows[0:1, :], in_=b_ih.rearrange("(o n) -> o n", o=1))
-        nc.sync.dma_start(out=bias_rows[1:2, :], in_=b_hh.rearrange("(o n) -> o n", o=1))
-        nc.sync.dma_start(out=bias_rows[2:3, 0:H], in_=z_bias.rearrange("(o n) -> o n", o=1))
-        nc.sync.dma_start(out=bias_rows[2:3, H : 2 * H], in_=m_bias.rearrange("(o n) -> o n", o=1))
-        nc.sync.dma_start(out=lam_rows[0:1, :], in_=log_lambda.rearrange("(o n) -> o n", o=1))
+        m_rows = const.tile([P, P], BF16)
+        nc.vector.memset(m_rows[:].bitcast(I32), 0)
+        nc.sync.dma_start(out=z_rows[0:1, :], in_=as_row(b_ih[0:H]))
+        nc.sync.dma_start(out=z_rows[1:2, :], in_=as_row(b_hh[0:H]))
+        nc.sync.dma_start(out=z_rows[2:3, :], in_=as_row(z_bias))
+        nc.sync.dma_start(out=m_rows[0:BLOCKS, :], in_=as_blocks(b_ih[H : 2 * H]))
+        nc.sync.dma_start(out=m_rows[BLOCKS : 2 * BLOCKS, :], in_=as_blocks(b_hh[H : 2 * H]))
+        nc.sync.dma_start(out=m_rows[2 * BLOCKS : 3 * BLOCKS, :], in_=as_blocks(m_bias))
+        nc.sync.dma_start(out=lam_rows[0:1, :], in_=as_row(log_lambda))
 
         load_cell(0)
         for c in range(1, AHEAD):
             load_chunk(c)
             load_cell(c)
 
-        bias_bc = const.tile([P, 2 * H], F32)
-        for g in range(2):
-            cols = slice(g * H, (g + 1) * H)
-            spread = psum_acc.tile([P, H], F32, tag="acc_z")
-            nc.tensor.matmul(out=spread[:], lhsT=ones[:], rhs=bias_rows[:, cols], start=True, stop=True)
-            nc.vector.tensor_copy(out=bias_bc[:, cols], in_=spread[:])
-        lam_bc = psum_acc.tile([P, H], F32, tag="acc_m")
-        nc.tensor.matmul(out=lam_bc[:], lhsT=ones[:], rhs=lam_rows[:], start=True, stop=True)
+        z_spread = psum.tile([P, H], F32, tag="acc_z")
+        nc.tensor.matmul(out=z_spread[:], lhsT=ones[:], rhs=z_rows[:], start=True, stop=True)
+        bias_z = const.tile([P, H], F32)
+        nc.vector.tensor_copy(out=bias_z[:], in_=z_spread[:])
+        lam_spread = psum.tile([P, H], F32, tag="acc_z")
+        nc.tensor.matmul(out=lam_spread[:], lhsT=ones[:], rhs=lam_rows[:], start=True, stop=True)
         decay = const.tile([P, H], F32)
-        nc.scalar.activation(out=decay[:], in_=lam_bc[:], func=ACT.Exp)
-        decay_m = const.tile([P, H], F32)
-        nc.scalar.mul(decay_m[:], decay[:], M_SCALE)
+        nc.scalar.activation(out=decay[:], in_=lam_spread[:], func=ACT.Exp)
+        m_turned = psum.tile([P, P], BF16, tag="back")
+        nc.tensor.transpose(m_turned[:], m_rows[:], ident_bf[:])
+        m_cols = const.tile([P, 3 * BLOCKS], F32)
+        nc.vector.tensor_copy(out=m_cols[:], in_=m_turned[:, 0 : 3 * BLOCKS])
+        bias_m = const.tile([P, BLOCKS], F32)
+        nc.vector.tensor_tensor(out=bias_m[:], in0=m_cols[:, 0:BLOCKS], in1=m_cols[:, BLOCKS : 2 * BLOCKS], op=ADD)
+        nc.vector.tensor_tensor(out=bias_m[:], in0=bias_m[:], in1=m_cols[:, 2 * BLOCKS : 3 * BLOCKS], op=ADD)
 
-        def transpose_tile(i):
-            c, r = divmod(i, CHUNK)
-            turned = psum_tr.tile([P, 2, 2, P], F32)
-            for a, name in enumerate(("x", "h")):
-                as_words = live[name, c][:, r, :].bitcast(F32)
-                for u in range(2):
-                    nc.tensor.transpose(turned[:, a, u, :], as_words[:, u : K // 2 : 2], ident[:])
-            live["turned", i] = turned
-
-        def regroup_tile(i):
-            grouped = front.tile([P, 2, P, 4], BF16, align_bytes=64)
-            nc.scalar.copy(
-                out=grouped[:].bitcast(F32),
-                in_=live["turned", i][:].rearrange("p a u r -> p a r u"),
-            )
-            live["grouped", i] = grouped
-
-        def quantise_tile(i):
-            codes = front.tile([P, 2, P], U32, align_bytes=64)
-            scales = front.tile([P, 2, P], U8, align_bytes=64)
-            nc.vector.quantize_mx(
-                out=codes[:].rearrange("p a r -> p (a r)").bitcast(FP8X4),
-                scales=scales[:].rearrange("p a r -> p (a r)"),
-                in_=live["grouped", i][:].rearrange("p a r t -> p (a r t)"),
-            )
-            live["codes", i] = codes
-            live["scales", i] = scales
-
-        def multiply_tile(i):
-            acc_z = psum_acc.tile([P, H], F32)
-            acc_m = psum_acc.tile([P, H], F32)
-            for g, acc in enumerate((acc_z, acc_m)):
+        def quantise_chunk(c):
+            grouped = work.tile([P, 2, ROWS, 4], BF16, align_bytes=64)
+            codes = work.tile([P, 2, ROWS], U32, align_bytes=64)
+            scales = work.tile([P, 2, ROWS], U8, align_bytes=64)
+            for r in range(CHUNK):
+                batch = slice(r * P, (r + 1) * P)
+                turned = psum.tile([P, 2, 2, P], F32)
                 for a, name in enumerate(("x", "h")):
-                    nc.tensor.matmul_mx(
-                        out=acc[:],
-                        lhsT=live["codes", i][:, a, :].bitcast(FP8X4),
-                        lhsT_scale=live["scales", i][:, a, :],
-                        rhs=words[name][:, 2 * g * H : 2 * (g + 1) * H].bitcast(FP4X4),
-                        rhs_scale=planes[name][:, g * H : (g + 1) * H],
-                        start=(a == 0),
-                        stop=(a == 1),
+                    as_words = live[name, c][:, r, :].bitcast(F32)
+                    for u in range(2):
+                        nc.tensor.transpose(turned[:, a, u, :], as_words[:, u : K // 2 : 2], ident[:])
+                nc.scalar.copy(
+                    out=grouped[:, :, batch, :].bitcast(F32),
+                    in_=turned[:].rearrange("p a u r -> p a r u"),
+                )
+                for a in range(2):
+                    nc.vector.quantize_mx(
+                        out=codes[:, a, batch].bitcast(FP8X4),
+                        scales=scales[:, a, batch],
+                        in_=grouped[:, a, batch, :].rearrange("p r t -> p (r t)"),
                     )
-            live["acc_z", i] = acc_z
-            live["acc_m", i] = acc_m
-
-        def add_bias_tile(i):
-            pre = middle.tile([P, 2 * H], F32)
-            nc.vector.tensor_tensor(out=pre[:, 0:H], in0=live["acc_z", i][:], in1=bias_bc[:, 0:H], op=ADD)
-            nc.vector.tensor_tensor(out=pre[:, H : 2 * H], in0=live["acc_m", i][:], in1=bias_bc[:, H : 2 * H], op=ADD)
-            live["pre", i] = pre
-
-        def squash_tile(i):
-            c, r = divmod(i, CHUNK)
-            if r == 0:
-                z_st = stores.tile([P, CHUNK, H], F32)
-                m_st = stores.tile([P, CHUNK, H], F32)
-                live["z", c] = z_st
-                live["m", c] = m_st
-            tanh_m = middle.tile([P, H], F32)
-            nc.scalar.activation(out=tanh_m[:], in_=live["pre", i][:, H : 2 * H], func=ACT.Tanh)
-            nc.scalar.activation(out=live["z", c][:, r, :], in_=live["pre", i][:, 0:H], func=ACT.Tanh)
-            nc.scalar.mul(live["m", c][:, r, :], tanh_m[:], M_SCALE)
-            live["tanh_m", i] = tanh_m
-
-        def scale_cell(c):
-            damped = middle.tile([P, CHUNK, H], F32)
-            nc.gpsimd.tensor_tensor(
+            live["codes", c] = codes
+            live["scales", c] = scales
+            damped = work.tile([P, CHUNK, H], F32, bufs=3)
+            nc.vector.tensor_tensor(
                 out=damped[:],
                 in0=live["c", c][:],
-                in1=decay_m[:].unsqueeze(1).to_broadcast([P, CHUNK, H]),
+                in1=decay[:].unsqueeze(1).to_broadcast([P, CHUNK, H]),
                 op=MULT,
             )
             live["damped", c] = damped
 
-        def product_tile(i):
-            c, r = divmod(i, CHUNK)
-            if r == 0:
-                i_st = stores.tile([P, CHUNK, H], F32)
-                live["i", c] = i_st
-            nc.vector.tensor_tensor(
-                out=live["i", c][:, r, :], in0=live["tanh_m", i][:], in1=live["damped", c][:, r, :], op=MULT
-            )
+        def gates_chunk(c):
+            codes = live["codes", c]
+            scales = live["scales", c]
+            tanh_t = work.tile([P, BLOCKS, ROWS], F32)
+            for j in range(BLOCKS):
+                acc_t = psum.tile([P, ROWS], F32)
+                for a, name in enumerate(("x", "h")):
+                    nc.tensor.matmul_mx(
+                        out=acc_t[:],
+                        lhsT=words[name][:, 2 * (H + j * P) : 2 * (H + (j + 1) * P)].bitcast(FP4X4),
+                        lhsT_scale=planes[name][:, H + j * P : H + (j + 1) * P],
+                        rhs=codes[:, a, :].bitcast(FP8X4),
+                        rhs_scale=scales[:, a, :],
+                        start=(a == 0),
+                        stop=(a == 1),
+                    )
+                nc.scalar.activation(out=tanh_t[:, j, :], in_=acc_t[:], func=ACT.Tanh, bias=bias_m[:, j : j + 1])
+            z_st = stores.tile([P, CHUNK, H], F32)
+            for r in range(CHUNK):
+                batch = slice(r * P, (r + 1) * P)
+                acc_z = psum.tile([P, H], F32)
+                for a, name in enumerate(("x", "h")):
+                    nc.tensor.matmul_mx(
+                        out=acc_z[:],
+                        lhsT=codes[:, a, batch].bitcast(FP8X4),
+                        lhsT_scale=scales[:, a, batch],
+                        rhs=words[name][:, 0 : 2 * H].bitcast(FP4X4),
+                        rhs_scale=planes[name][:, 0:H],
+                        start=(a == 0),
+                        stop=(a == 1),
+                    )
+                pre_z = work.tile([P, H], F32)
+                nc.vector.tensor_tensor(out=pre_z[:], in0=acc_z[:], in1=bias_z[:], op=ADD)
+                nc.scalar.activation(out=z_st[:, r, :], in_=pre_z[:], func=ACT.Tanh)
+            live["z", c] = z_st
+            live["tanh_t", c] = tanh_t
 
-        def sum_tile(i):
-            c, r = divmod(i, CHUNK)
-            nc.vector.tensor_tensor(
-                out=live["i", c][:, r, :], in0=live["i", c][:, r, :], in1=live["z", c][:, r, :], op=ADD
-            )
-            if r == CHUNK - 1:
-                rows = slice(c * CHUNK, (c + 1) * CHUNK)
-                nc.sync.dma_start(out=z_v[:, rows, :], in_=live["z", c][:])
-                nc.sync.dma_start(out=m_v[:, rows, :], in_=live["m", c][:])
-                nc.sync.dma_start(out=i_v[:, rows, :], in_=live["i", c][:])
+        def finish_chunk(c):
+            z_st = live["z", c]
+            tanh_t = live["tanh_t", c]
+            damped = live["damped", c]
+            m_st = stores.tile([P, CHUNK, H], F32)
+            i_st = stores.tile([P, CHUNK, H], F32)
+            for r in range(CHUNK):
+                back = psum.tile([P, H], F32)
+                for j in range(BLOCKS):
+                    nc.tensor.transpose(back[:, j * P : (j + 1) * P], tanh_t[:, j, r * P : (r + 1) * P], ident[:])
+                nc.scalar.mul(m_st[:, r, :], back[:], M_SCALE)
+                nc.vector.tensor_tensor(out=i_st[:, r, :], in0=m_st[:, r, :], in1=damped[:, r, :], op=MULT)
+                nc.vector.tensor_tensor(out=i_st[:, r, :], in0=i_st[:, r, :], in1=z_st[:, r, :], op=ADD)
+                if c == CHUNKS - 1:
+                    first = r
+                elif r == CHUNK - 1:
+                    first = 0
+                else:
+                    continue
+                done = slice(first, r + 1)
+                rows = slice(c * CHUNK + first, c * CHUNK + r + 1)
+                nc.sync.dma_start(out=z_v[:, rows, :], in_=z_st[:, done, :])
+                nc.sync.dma_start(out=m_v[:, rows, :], in_=m_st[:, done, :])
+                nc.sync.dma_start(out=i_v[:, rows, :], in_=i_st[:, done, :])
 
-        for j in range(TILES + 4):
-            if j < TILES and j % CHUNK == 0:
-                c = j // CHUNK
-                if c + AHEAD < CHUNKS:
-                    load_chunk(c + AHEAD)
-                    load_cell(c + AHEAD)
-                scale_cell(c)
-            if j < TILES:
-                transpose_tile(j)
-            if 0 <= j - 4 < TILES:
-                product_tile(j - 4)
-            if 0 <= j - 1 < TILES:
-                quantise_tile(j - 1)
-                multiply_tile(j - 1)
-            if 0 <= j - 4 < TILES:
-                sum_tile(j - 4)
-            if 0 <= j - 2 < TILES:
-                add_bias_tile(j - 2)
-            if 0 <= j - 3 < TILES:
-                squash_tile(j - 3)
-            if j < TILES:
-                regroup_tile(j)
+        for s in range(CHUNKS + 2):
+            if s + AHEAD < CHUNKS:
+                load_chunk(s + AHEAD)
+                load_cell(s + AHEAD)
+            if s < CHUNKS:
+                quantise_chunk(s)
+            if 0 <= s - 1 < CHUNKS:
+                gates_chunk(s - 1)
+            if 0 <= s - 2 < CHUNKS:
+                finish_chunk(s - 2)

@@ -24,7 +24,19 @@ CHUNK = 4
 ROWS = CHUNK * P
 CHUNKS = TILES // CHUNK
 BLOCKS = H // P
-AHEAD = 3
+assert BLOCKS == CHUNK
+
+QUANTISE = 1
+Z_MULTIPLY = 2
+Z_BIAS = 3
+Z_TANH = 4
+M_MULTIPLY = 5
+M_TANH = 6
+TURN_BACK = 10
+M_OUT = 11
+DAMP = 11
+PRODUCT = 12
+STEPS = TILES + PRODUCT
 
 FLOPS = 2 * BATCH * (2 * K) * (2 * H)
 
@@ -63,35 +75,35 @@ def tile_koslmcell_pa_t_kernel(
         return vector.rearrange("(j p) -> j p", p=P)
 
     with ExitStack() as ctx:
+        ctx.enter_context(tc.manual_schedule())
         const = ctx.enter_context(tc.tile_pool(name="const", bufs=1))
-        loads = ctx.enter_context(tc.tile_pool(name="loads", bufs=AHEAD + 1))
+        inputs = ctx.enter_context(tc.tile_pool(name="inputs", bufs=1))
         work = ctx.enter_context(tc.tile_pool(name="work", bufs=2))
-        stores = ctx.enter_context(tc.tile_pool(name="stores", bufs=3))
+        stores = ctx.enter_context(tc.tile_pool(name="stores", bufs=2))
         psum = ctx.enter_context(tc.psum_pool(name="psum", bufs=2))
 
         live = {}
 
-        def load_chunk(c):
-            rows = slice(c * CHUNK, (c + 1) * CHUNK)
-            x_sb = loads.tile([P, CHUNK, K], BF16)
-            nc.sync.dma_start(out=x_sb[:], in_=x_v[:, rows, :])
-            h_sb = loads.tile([P, CHUNK, K], BF16)
-            nc.sync.dma_start(out=h_sb[:], in_=h_v[:, rows, :])
-            live["x", c] = x_sb
-            live["h", c] = h_sb
+        def load(name, view, c):
+            held = inputs.tile([P, CHUNK, K], BF16, name="%s%d" % (name, c))
+            nc.sync.dma_start(out=held[:], in_=view[:, c * CHUNK : (c + 1) * CHUNK, :])
+            live[name, c] = held
 
-        def load_cell(c):
-            rows = slice(c * CHUNK, (c + 1) * CHUNK)
-            c_sb = loads.tile([P, CHUNK, H], BF16)
-            nc.sync.dma_start(out=c_sb[:], in_=c_v[:, rows, :])
-            live["c", c] = c_sb
+        load("x", x_v, 0)
+        load("h", h_v, 0)
 
-        load_chunk(0)
-
-        ident = const.tile([P, P], F32)
-        make_identity(nc, ident[:])
-        ident_bf = const.tile([P, P], BF16)
-        make_identity(nc, ident_bf[:])
+        z_rows = const.tile([P, H], BF16)
+        nc.vector.memset(z_rows[:].bitcast(I32), 0)
+        m_rows = const.tile([P, P], BF16)
+        nc.vector.memset(m_rows[:].bitcast(I32), 0)
+        lam_row = const.tile([1, H], BF16)
+        nc.scalar.dma_start(out=lam_row[:], in_=as_row(log_lambda))
+        nc.scalar.dma_start(out=z_rows[0:1, :], in_=as_row(b_ih[0:H]))
+        nc.scalar.dma_start(out=z_rows[1:2, :], in_=as_row(b_hh[0:H]))
+        nc.scalar.dma_start(out=z_rows[2:3, :], in_=as_row(z_bias))
+        nc.scalar.dma_start(out=m_rows[0:BLOCKS, :], in_=as_blocks(b_ih[H : 2 * H]))
+        nc.scalar.dma_start(out=m_rows[BLOCKS : 2 * BLOCKS, :], in_=as_blocks(b_hh[H : 2 * H]))
+        nc.scalar.dma_start(out=m_rows[2 * BLOCKS : 3 * BLOCKS, :], in_=as_blocks(m_bias))
 
         words = {}
         planes = {}
@@ -108,144 +120,191 @@ def tile_koslmcell_pa_t_kernel(
             words[name] = w_sb
             planes[name] = plane
 
-        ones = const.tile([P, P], BF16)
+        for c in range(1, CHUNKS):
+            load("x", x_v, c)
+            load("h", h_v, c)
+        for c in range(CHUNKS):
+            load("c", c_v, c)
+
+        ident = const.tile([P, P], F32)
+        make_identity(nc, ident[:])
+        ident_bf = const.tile([P, P], BF16)
+        make_identity(nc, ident_bf[:])
+        ones_bf = const.tile([P, P], BF16)
+        nc.vector.memset(ones_bf[:], 1.0)
+        ones = const.tile([P, P], F32)
         nc.vector.memset(ones[:], 1.0)
-        z_rows = const.tile([P, H], BF16)
-        nc.vector.memset(z_rows[:].bitcast(I32), 0)
-        lam_rows = const.tile([P, H], BF16)
-        nc.vector.memset(lam_rows[:].bitcast(I32), 0)
-        m_rows = const.tile([P, P], BF16)
-        nc.vector.memset(m_rows[:].bitcast(I32), 0)
-        nc.sync.dma_start(out=z_rows[0:1, :], in_=as_row(b_ih[0:H]))
-        nc.sync.dma_start(out=z_rows[1:2, :], in_=as_row(b_hh[0:H]))
-        nc.sync.dma_start(out=z_rows[2:3, :], in_=as_row(z_bias))
-        nc.sync.dma_start(out=m_rows[0:BLOCKS, :], in_=as_blocks(b_ih[H : 2 * H]))
-        nc.sync.dma_start(out=m_rows[BLOCKS : 2 * BLOCKS, :], in_=as_blocks(b_hh[H : 2 * H]))
-        nc.sync.dma_start(out=m_rows[2 * BLOCKS : 3 * BLOCKS, :], in_=as_blocks(m_bias))
-        nc.sync.dma_start(out=lam_rows[0:1, :], in_=as_row(log_lambda))
+        decay_rows = const.tile([P, H], F32)
+        nc.vector.memset(decay_rows[:].bitcast(I32), 0)
 
-        load_cell(0)
-        for c in range(1, AHEAD):
-            load_chunk(c)
-            load_cell(c)
-
-        z_spread = psum.tile([P, H], F32, tag="acc_z")
-        nc.tensor.matmul(out=z_spread[:], lhsT=ones[:], rhs=z_rows[:], start=True, stop=True)
         bias_z = const.tile([P, H], F32)
-        nc.vector.tensor_copy(out=bias_z[:], in_=z_spread[:])
-        lam_spread = psum.tile([P, H], F32, tag="acc_z")
-        nc.tensor.matmul(out=lam_spread[:], lhsT=ones[:], rhs=lam_rows[:], start=True, stop=True)
-        decay = const.tile([P, H], F32)
-        nc.scalar.activation(out=decay[:], in_=lam_spread[:], func=ACT.Exp)
-        m_turned = psum.tile([P, P], BF16, tag="back")
-        nc.tensor.transpose(m_turned[:], m_rows[:], ident_bf[:])
-        m_cols = const.tile([P, 3 * BLOCKS], F32)
-        nc.vector.tensor_copy(out=m_cols[:], in_=m_turned[:, 0 : 3 * BLOCKS])
         bias_m = const.tile([P, BLOCKS], F32)
-        nc.vector.tensor_tensor(out=bias_m[:], in0=m_cols[:, 0:BLOCKS], in1=m_cols[:, BLOCKS : 2 * BLOCKS], op=ADD)
-        nc.vector.tensor_tensor(out=bias_m[:], in0=bias_m[:], in1=m_cols[:, 2 * BLOCKS : 3 * BLOCKS], op=ADD)
+        decay = psum.tile([P, H], F32, bufs=1)
 
-        def quantise_chunk(c):
-            grouped = work.tile([P, 2, ROWS, 4], BF16, align_bytes=64)
-            codes = work.tile([P, 2, ROWS], U32, align_bytes=64)
-            scales = work.tile([P, 2, ROWS], U8, align_bytes=64)
-            for r in range(CHUNK):
-                batch = slice(r * P, (r + 1) * P)
-                turned = psum.tile([P, 2, 2, P], F32)
-                for a, name in enumerate(("x", "h")):
-                    as_words = live[name, c][:, r, :].bitcast(F32)
-                    for u in range(2):
-                        nc.tensor.transpose(turned[:, a, u, :], as_words[:, u : K // 2 : 2], ident[:])
-                nc.scalar.copy(
-                    out=grouped[:, :, batch, :].bitcast(F32),
-                    in_=turned[:].rearrange("p a u r -> p a r u"),
-                )
-                for a in range(2):
-                    nc.vector.quantize_mx(
-                        out=codes[:, a, batch].bitcast(FP8X4),
-                        scales=scales[:, a, batch],
-                        in_=grouped[:, a, batch, :].rearrange("p r t -> p (r t)"),
-                    )
-            live["codes", c] = codes
-            live["scales", c] = scales
-            damped = work.tile([P, CHUNK, H], F32, bufs=3)
-            nc.vector.tensor_tensor(
-                out=damped[:],
-                in0=live["c", c][:],
-                in1=decay[:].unsqueeze(1).to_broadcast([P, CHUNK, H]),
-                op=MULT,
+        def spread_decay():
+            nc.tensor.matmul(out=decay[:], lhsT=ones[:], rhs=decay_rows[:], start=True, stop=True)
+
+        def spread_biases():
+            nc.scalar.activation(out=decay_rows[0:1, :], in_=lam_row[:], func=ACT.Exp)
+            z_spread = psum.tile([P, H], F32, tag="acc_z")
+            nc.tensor.matmul(out=z_spread[:], lhsT=ones_bf[:], rhs=z_rows[:], start=True, stop=True)
+            nc.vector.tensor_copy(out=bias_z[:], in_=z_spread[:])
+            m_turned = psum.tile([P, P], BF16, tag="back")
+            nc.tensor.transpose(m_turned[:], m_rows[:], ident_bf[:])
+            m_cols = const.tile([P, 3 * BLOCKS], F32)
+            nc.vector.tensor_copy(out=m_cols[:], in_=m_turned[:, 0 : 3 * BLOCKS])
+            nc.vector.tensor_tensor(out=bias_m[:], in0=m_cols[:, 0:BLOCKS], in1=m_cols[:, BLOCKS : 2 * BLOCKS], op=ADD)
+            nc.vector.tensor_tensor(out=bias_m[:], in0=bias_m[:], in1=m_cols[:, 2 * BLOCKS : 3 * BLOCKS], op=ADD)
+
+        def transpose_tile(i):
+            c, r = divmod(i, CHUNK)
+            turned = psum.tile([P, 2, 2, P], F32)
+            for a, name in enumerate(("x", "h")):
+                as_words = live[name, c][:, r, :].bitcast(F32)
+                for u in range(2):
+                    nc.tensor.transpose(turned[:, a, u, :], as_words[:, u : K // 2 : 2], ident[:])
+            live["turned", i] = turned
+
+        def regroup_tile(i):
+            c, r = divmod(i, CHUNK)
+            if r == 0:
+                grouped = work.tile([P, 2, ROWS, 4], BF16, align_bytes=64)
+                live["grouped", c] = grouped
+            nc.scalar.copy(
+                out=live["grouped", c][:, :, r * P : (r + 1) * P, :].bitcast(F32),
+                in_=live["turned", i][:].rearrange("p a u r -> p a r u"),
             )
-            live["damped", c] = damped
 
-        def gates_chunk(c):
-            codes = live["codes", c]
-            scales = live["scales", c]
-            tanh_t = work.tile([P, BLOCKS, ROWS], F32)
+        def quantise_tile(i):
+            c, r = divmod(i, CHUNK)
+            if r == 0:
+                codes = work.tile([P, 2, ROWS], U32, align_bytes=64)
+                scales = work.tile([P, 2, ROWS], U8, align_bytes=64)
+                live["codes", c] = codes
+                live["scales", c] = scales
+            batch = slice(r * P, (r + 1) * P)
+            for a in range(2):
+                nc.vector.quantize_mx(
+                    out=live["codes", c][:, a, batch].bitcast(FP8X4),
+                    scales=live["scales", c][:, a, batch],
+                    in_=live["grouped", c][:, a, batch, :].rearrange("p r t -> p (r t)"),
+                )
+
+        def multiply_z(i):
+            c, r = divmod(i, CHUNK)
+            batch = slice(r * P, (r + 1) * P)
+            acc_z = psum.tile([P, H], F32)
+            for a, name in enumerate(("x", "h")):
+                nc.tensor.matmul_mx(
+                    out=acc_z[:],
+                    lhsT=live["codes", c][:, a, batch].bitcast(FP8X4),
+                    lhsT_scale=live["scales", c][:, a, batch],
+                    rhs=words[name][:, 0 : 2 * H].bitcast(FP4X4),
+                    rhs_scale=planes[name][:, 0:H],
+                    start=(a == 0),
+                    stop=(a == 1),
+                )
+            live["acc_z", i] = acc_z
+
+        def add_bias_z(i):
+            pre_z = work.tile([P, H], F32, bufs=3)
+            nc.vector.tensor_tensor(out=pre_z[:], in0=live["acc_z", i][:], in1=bias_z[:], op=ADD)
+            live["pre_z", i] = pre_z
+
+        def tanh_z(i):
+            c, r = divmod(i, CHUNK)
+            if r == 0:
+                z_st = stores.tile([P, CHUNK, H], F32, bufs=4)
+                live["z", c] = z_st
+            nc.scalar.activation(out=live["z", c][:, r, :], in_=live["pre_z", i][:], func=ACT.Tanh)
+            if r == CHUNK - 1:
+                nc.sync.dma_start(out=z_v[:, c * CHUNK : (c + 1) * CHUNK, :], in_=live["z", c][:])
+
+        def multiply_m(b):
+            c, j = divmod(b, BLOCKS)
+            acc_t = psum.tile([P, ROWS], F32, bufs=1)
+            for a, name in enumerate(("x", "h")):
+                nc.tensor.matmul_mx(
+                    out=acc_t[:],
+                    lhsT=words[name][:, 2 * (H + j * P) : 2 * (H + (j + 1) * P)].bitcast(FP4X4),
+                    lhsT_scale=planes[name][:, H + j * P : H + (j + 1) * P],
+                    rhs=live["codes", c][:, a, :].bitcast(FP8X4),
+                    rhs_scale=live["scales", c][:, a, :],
+                    start=(a == 0),
+                    stop=(a == 1),
+                )
+            live["acc_t", b] = acc_t
+
+        def tanh_m(b):
+            c, j = divmod(b, BLOCKS)
+            if j == 0:
+                tanh_t = work.tile([P, BLOCKS, ROWS], F32)
+                live["tanh_t", c] = tanh_t
+            nc.scalar.activation(
+                out=live["tanh_t", c][:, j, :], in_=live["acc_t", b][:], func=ACT.Tanh, bias=bias_m[:, j : j + 1]
+            )
+
+        def turn_back(i):
+            c, r = divmod(i, CHUNK)
+            back = psum.tile([P, H], F32)
             for j in range(BLOCKS):
-                acc_t = psum.tile([P, ROWS], F32)
-                for a, name in enumerate(("x", "h")):
-                    nc.tensor.matmul_mx(
-                        out=acc_t[:],
-                        lhsT=words[name][:, 2 * (H + j * P) : 2 * (H + (j + 1) * P)].bitcast(FP4X4),
-                        lhsT_scale=planes[name][:, H + j * P : H + (j + 1) * P],
-                        rhs=codes[:, a, :].bitcast(FP8X4),
-                        rhs_scale=scales[:, a, :],
-                        start=(a == 0),
-                        stop=(a == 1),
-                    )
-                nc.scalar.activation(out=tanh_t[:, j, :], in_=acc_t[:], func=ACT.Tanh, bias=bias_m[:, j : j + 1])
-            z_st = stores.tile([P, CHUNK, H], F32)
-            for r in range(CHUNK):
-                batch = slice(r * P, (r + 1) * P)
-                acc_z = psum.tile([P, H], F32)
-                for a, name in enumerate(("x", "h")):
-                    nc.tensor.matmul_mx(
-                        out=acc_z[:],
-                        lhsT=codes[:, a, batch].bitcast(FP8X4),
-                        lhsT_scale=scales[:, a, batch],
-                        rhs=words[name][:, 0 : 2 * H].bitcast(FP4X4),
-                        rhs_scale=planes[name][:, 0:H],
-                        start=(a == 0),
-                        stop=(a == 1),
-                    )
-                pre_z = work.tile([P, H], F32)
-                nc.vector.tensor_tensor(out=pre_z[:], in0=acc_z[:], in1=bias_z[:], op=ADD)
-                nc.scalar.activation(out=z_st[:, r, :], in_=pre_z[:], func=ACT.Tanh)
-            live["z", c] = z_st
-            live["tanh_t", c] = tanh_t
+                nc.tensor.transpose(back[:, j * P : (j + 1) * P], live["tanh_t", c][:, j, r * P : (r + 1) * P], ident[:])
+            live["back", i] = back
 
-        def finish_chunk(c):
-            z_st = live["z", c]
-            tanh_t = live["tanh_t", c]
-            damped = live["damped", c]
-            m_st = stores.tile([P, CHUNK, H], F32)
-            i_st = stores.tile([P, CHUNK, H], F32)
-            for r in range(CHUNK):
-                back = psum.tile([P, H], F32)
-                for j in range(BLOCKS):
-                    nc.tensor.transpose(back[:, j * P : (j + 1) * P], tanh_t[:, j, r * P : (r + 1) * P], ident[:])
-                nc.scalar.mul(m_st[:, r, :], back[:], M_SCALE)
-                nc.vector.tensor_tensor(out=i_st[:, r, :], in0=m_st[:, r, :], in1=damped[:, r, :], op=MULT)
-                nc.vector.tensor_tensor(out=i_st[:, r, :], in0=i_st[:, r, :], in1=z_st[:, r, :], op=ADD)
-                if c == CHUNKS - 1:
-                    first = r
-                elif r == CHUNK - 1:
-                    first = 0
-                else:
-                    continue
-                done = slice(first, r + 1)
-                rows = slice(c * CHUNK + first, c * CHUNK + r + 1)
-                nc.sync.dma_start(out=z_v[:, rows, :], in_=z_st[:, done, :])
-                nc.sync.dma_start(out=m_v[:, rows, :], in_=m_st[:, done, :])
-                nc.sync.dma_start(out=i_v[:, rows, :], in_=i_st[:, done, :])
+        def store_tiles(view, held, c, r):
+            if c == CHUNKS - 1:
+                first = r
+            elif r == CHUNK - 1:
+                first = 0
+            else:
+                return
+            nc.sync.dma_start(out=view[:, c * CHUNK + first : c * CHUNK + r + 1, :], in_=held[:, first : r + 1, :])
 
-        for s in range(CHUNKS + 2):
-            if s + AHEAD < CHUNKS:
-                load_chunk(s + AHEAD)
-                load_cell(s + AHEAD)
-            if s < CHUNKS:
-                quantise_chunk(s)
-            if 0 <= s - 1 < CHUNKS:
-                gates_chunk(s - 1)
-            if 0 <= s - 2 < CHUNKS:
-                finish_chunk(s - 2)
+        def scale_m(i):
+            c, r = divmod(i, CHUNK)
+            if r == 0:
+                m_st = stores.tile([P, CHUNK, H], F32)
+                live["m", c] = m_st
+            nc.scalar.mul(live["m", c][:, r, :], live["back", i][:], M_SCALE)
+            store_tiles(m_v, live["m", c], c, r)
+
+        def damp_cell(i):
+            c, r = divmod(i, CHUNK)
+            damped = work.tile([P, H], F32, bufs=3)
+            nc.vector.tensor_tensor(out=damped[:], in0=live["c", c][:, r, :], in1=decay[:], op=MULT)
+            live["damped", i] = damped
+
+        def product(i):
+            c, r = divmod(i, CHUNK)
+            if r == 0:
+                i_st = stores.tile([P, CHUNK, H], F32)
+                live["i", c] = i_st
+            nc.vector.tensor_tensor(out=live["i", c][:, r, :], in0=live["m", c][:, r, :], in1=live["damped", i][:], op=MULT)
+
+        def total(i):
+            c, r = divmod(i, CHUNK)
+            nc.gpsimd.tensor_tensor(out=live["i", c][:, r, :], in0=live["i", c][:, r, :], in1=live["z", c][:, r, :], op=ADD)
+            store_tiles(i_v, live["i", c], c, r)
+
+        def run(stage, i):
+            if 0 <= i < TILES:
+                stage(i)
+
+        for s in range(STEPS):
+            run(transpose_tile, s)
+            run(turn_back, s - TURN_BACK)
+            run(multiply_m, s - M_MULTIPLY)
+            run(multiply_z, s - Z_MULTIPLY)
+            run(product, s - PRODUCT)
+            run(total, s - PRODUCT)
+            run(quantise_tile, s - QUANTISE)
+            run(add_bias_z, s - Z_BIAS)
+            run(damp_cell, s - DAMP)
+            run(tanh_m, s - M_TANH)
+            run(scale_m, s - M_OUT)
+            run(tanh_z, s - Z_TANH)
+            run(regroup_tile, s)
+            if s == 1:
+                spread_biases()
+            if s == 3:
+                spread_decay()

@@ -89,8 +89,13 @@ def tile_koslmcell_pa_t_kernel(
             nc.sync.dma_start(out=held[:], in_=view[:, c * CHUNK : (c + 1) * CHUNK, :])
             live[name, c] = held
 
-        load("x", x_v, 0)
-        load("h", h_v, 0)
+        x_first = inputs.tile([P, CHUNK, K], BF16)
+        h_first = inputs.tile([P, CHUNK, K], BF16)
+        for rows in (slice(0, 1), slice(1, CHUNK)):
+            nc.sync.dma_start(out=x_first[:, rows, :], in_=x_v[:, rows, :])
+            nc.sync.dma_start(out=h_first[:, rows, :], in_=h_v[:, rows, :])
+        live["x", 0] = x_first
+        live["h", 0] = h_first
 
         z_rows = const.tile([P, H], BF16)
         nc.vector.memset(z_rows[:].bitcast(I32), 0)
@@ -170,7 +175,8 @@ def tile_koslmcell_pa_t_kernel(
             if r == 0:
                 grouped = work.tile([P, 2, ROWS, 4], BF16, align_bytes=64)
                 live["grouped", c] = grouped
-            nc.scalar.copy(
+            mover = nc.vector.tensor_copy if r == CHUNK - 1 else nc.scalar.copy
+            mover(
                 out=live["grouped", c][:, :, r * P : (r + 1) * P, :].bitcast(F32),
                 in_=live["turned", i][:].rearrange("p a u r -> p a r u"),
             )
@@ -283,7 +289,8 @@ def tile_koslmcell_pa_t_kernel(
 
         def total(i):
             c, r = divmod(i, CHUNK)
-            nc.gpsimd.tensor_tensor(out=live["i", c][:, r, :], in0=live["i", c][:, r, :], in1=live["z", c][:, r, :], op=ADD)
+            adder = nc.vector if c == CHUNKS - 1 else nc.gpsimd
+            adder.tensor_tensor(out=live["i", c][:, r, :], in0=live["i", c][:, r, :], in1=live["z", c][:, r, :], op=ADD)
             store_tiles(i_v, live["i", c], c, r)
 
         def run(stage, i):

@@ -32,11 +32,12 @@ Z_BIAS = 3
 Z_TANH = 4
 M_MULTIPLY = 5
 M_TANH = 6
-TURN_BACK = 10
-M_OUT = 11
-DAMP = 11
-PRODUCT = 12
+TURN_BACK = 7
+M_OUT = 8
+PRODUCT = 9
+DAMP = 3
 STEPS = TILES + PRODUCT
+VECTOR_SUMS = 2
 
 FLOPS = 2 * BATCH * (2 * K) * (2 * H)
 
@@ -89,32 +90,16 @@ def tile_koslmcell_pa_t_kernel(
             nc.sync.dma_start(out=held[:], in_=view[:, c * CHUNK : (c + 1) * CHUNK, :])
             live[name, c] = held
 
-        x_first = inputs.tile([P, CHUNK, K], BF16)
-        h_first = inputs.tile([P, CHUNK, K], BF16)
-        for rows in (slice(0, 1), slice(1, CHUNK)):
-            nc.sync.dma_start(out=x_first[:, rows, :], in_=x_v[:, rows, :])
-            nc.sync.dma_start(out=h_first[:, rows, :], in_=h_v[:, rows, :])
-        live["x", 0] = x_first
-        live["h", 0] = h_first
-
-        z_rows = const.tile([P, H], BF16)
-        nc.vector.memset(z_rows[:].bitcast(I32), 0)
-        m_rows = const.tile([P, P], BF16)
-        nc.vector.memset(m_rows[:].bitcast(I32), 0)
-        lam_row = const.tile([1, H], BF16)
-        nc.scalar.dma_start(out=lam_row[:], in_=as_row(log_lambda))
-        nc.scalar.dma_start(out=z_rows[0:1, :], in_=as_row(b_ih[0:H]))
-        nc.scalar.dma_start(out=z_rows[1:2, :], in_=as_row(b_hh[0:H]))
-        nc.scalar.dma_start(out=z_rows[2:3, :], in_=as_row(z_bias))
-        nc.scalar.dma_start(out=m_rows[0:BLOCKS, :], in_=as_blocks(b_ih[H : 2 * H]))
-        nc.scalar.dma_start(out=m_rows[BLOCKS : 2 * BLOCKS, :], in_=as_blocks(b_hh[H : 2 * H]))
-        nc.scalar.dma_start(out=m_rows[2 * BLOCKS : 3 * BLOCKS, :], in_=as_blocks(m_bias))
+        load("x", x_v, 0)
+        load("h", h_v, 0)
 
         words = {}
         planes = {}
-        for name, w_words, w_scales in (("x", W_ih_words, W_ih_scales), ("h", W_hh_words, W_hh_scales)):
+        for name, w_words in (("x", W_ih_words), ("h", W_hh_words)):
             w_sb = const.tile([P, 4 * H], U8, name="words_" + name, align_bytes=64)
             nc.sync.dma_start(out=w_sb[:].bitcast(I32), in_=w_words[0].bitcast(I32))
+            words[name] = w_sb
+        for name, w_scales in (("x", W_ih_scales), ("h", W_hh_scales)):
             plane = const.tile([P, 2 * H], U8, name="plane_" + name, align_bytes=64)
             nc.vector.memset(plane[:].bitcast(I32), 0)
             for quad in range(4):
@@ -122,13 +107,24 @@ def tile_koslmcell_pa_t_kernel(
                     out=plane[32 * quad : 32 * quad + 4, :].bitcast(I32),
                     in_=w_scales[0, 4 * quad : 4 * quad + 4, :].bitcast(I32),
                 )
-            words[name] = w_sb
             planes[name] = plane
 
+        z_rows = const.tile([P, H], BF16)
+        nc.vector.memset(z_rows[:].bitcast(I32), 0)
+        m_rows = const.tile([P, P], BF16)
+        nc.vector.memset(m_rows[:].bitcast(I32), 0)
+        lam_row = const.tile([1, H], BF16)
+        nc.sync.dma_start(out=lam_row[:], in_=as_row(log_lambda))
+        nc.sync.dma_start(out=z_rows[0:1, :], in_=as_row(b_ih[0:H]))
+        nc.sync.dma_start(out=z_rows[1:2, :], in_=as_row(b_hh[0:H]))
+        nc.sync.dma_start(out=z_rows[2:3, :], in_=as_row(z_bias))
+        load("c", c_v, 0)
+        nc.sync.dma_start(out=m_rows[0:BLOCKS, :], in_=as_blocks(b_ih[H : 2 * H]))
+        nc.sync.dma_start(out=m_rows[BLOCKS : 2 * BLOCKS, :], in_=as_blocks(b_hh[H : 2 * H]))
+        nc.sync.dma_start(out=m_rows[2 * BLOCKS : 3 * BLOCKS, :], in_=as_blocks(m_bias))
         for c in range(1, CHUNKS):
             load("x", x_v, c)
             load("h", h_v, c)
-        for c in range(CHUNKS):
             load("c", c_v, c)
 
         ident = const.tile([P, P], F32)
@@ -150,10 +146,11 @@ def tile_koslmcell_pa_t_kernel(
             nc.tensor.matmul(out=decay[:], lhsT=ones[:], rhs=decay_rows[:], start=True, stop=True)
 
         def spread_biases():
-            nc.scalar.activation(out=decay_rows[0:1, :], in_=lam_row[:], func=ACT.Exp)
             z_spread = psum.tile([P, H], F32, tag="acc_z")
             nc.tensor.matmul(out=z_spread[:], lhsT=ones_bf[:], rhs=z_rows[:], start=True, stop=True)
             nc.vector.tensor_copy(out=bias_z[:], in_=z_spread[:])
+
+        def turn_m_bias():
             m_turned = psum.tile([P, P], BF16, tag="back")
             nc.tensor.transpose(m_turned[:], m_rows[:], ident_bf[:])
             m_cols = const.tile([P, 3 * BLOCKS], F32)
@@ -171,15 +168,9 @@ def tile_koslmcell_pa_t_kernel(
             live["turned", i] = turned
 
         def regroup_tile(i):
-            c, r = divmod(i, CHUNK)
-            if r == 0:
-                grouped = work.tile([P, 2, ROWS, 4], BF16, align_bytes=64)
-                live["grouped", c] = grouped
-            mover = nc.vector.tensor_copy if r == CHUNK - 1 else nc.scalar.copy
-            mover(
-                out=live["grouped", c][:, :, r * P : (r + 1) * P, :].bitcast(F32),
-                in_=live["turned", i][:].rearrange("p a u r -> p a r u"),
-            )
+            grouped = work.tile([P, 2, P, 4], BF16, bufs=3, align_bytes=64)
+            nc.scalar.copy(out=grouped[:].bitcast(F32), in_=live["turned", i][:].rearrange("p a u r -> p a r u"))
+            live["grouped", i] = grouped
 
         def quantise_tile(i):
             c, r = divmod(i, CHUNK)
@@ -193,7 +184,7 @@ def tile_koslmcell_pa_t_kernel(
                 nc.vector.quantize_mx(
                     out=live["codes", c][:, a, batch].bitcast(FP8X4),
                     scales=live["scales", c][:, a, batch],
-                    in_=live["grouped", c][:, a, batch, :].rearrange("p r t -> p (r t)"),
+                    in_=live["grouped", i][:, a, :, :].rearrange("p r t -> p (r t)"),
                 )
 
         def multiply_z(i):
@@ -220,10 +211,12 @@ def tile_koslmcell_pa_t_kernel(
         def tanh_z(i):
             c, r = divmod(i, CHUNK)
             if r == 0:
-                z_st = stores.tile([P, CHUNK, H], F32, bufs=4)
+                z_st = stores.tile([P, CHUNK, H], F32, bufs=3)
                 live["z", c] = z_st
             nc.scalar.activation(out=live["z", c][:, r, :], in_=live["pre_z", i][:], func=ACT.Tanh)
-            if r == CHUNK - 1:
+            if c == CHUNKS - 1:
+                nc.sync.dma_start(out=z_v[:, i : i + 1, :], in_=live["z", c][:, r : r + 1, :])
+            elif r == CHUNK - 1:
                 nc.sync.dma_start(out=z_v[:, c * CHUNK : (c + 1) * CHUNK, :], in_=live["z", c][:])
 
         def multiply_m(b):
@@ -242,56 +235,52 @@ def tile_koslmcell_pa_t_kernel(
             live["acc_t", b] = acc_t
 
         def tanh_m(b):
+            j = b % BLOCKS
+            tanh_t = work.tile([P, ROWS], F32, bufs=3)
+            nc.scalar.activation(out=tanh_t[:], in_=live["acc_t", b][:], func=ACT.Tanh, bias=bias_m[:, j : j + 1])
+            live["tanh_t", b] = tanh_t
+
+        def turn_back(b):
+            back = psum.tile([P, CHUNK, P], F32)
+            for r in range(CHUNK):
+                nc.tensor.transpose(back[:, r, :], live["tanh_t", b][:, r * P : (r + 1) * P], ident[:])
+            live["back", b] = back
+
+        def store_blocks(view, held, c, j):
+            width = BLOCKS // 2 if c == CHUNKS - 1 else BLOCKS
+            if (j + 1) % width == 0:
+                cols = slice((j + 1 - width) * P, (j + 1) * P)
+                nc.sync.dma_start(out=view[:, c * CHUNK : (c + 1) * CHUNK, cols], in_=held[:, :, cols])
+
+        def scale_m(b):
             c, j = divmod(b, BLOCKS)
             if j == 0:
-                tanh_t = work.tile([P, BLOCKS, ROWS], F32)
-                live["tanh_t", c] = tanh_t
-            nc.scalar.activation(
-                out=live["tanh_t", c][:, j, :], in_=live["acc_t", b][:], func=ACT.Tanh, bias=bias_m[:, j : j + 1]
-            )
-
-        def turn_back(i):
-            c, r = divmod(i, CHUNK)
-            back = psum.tile([P, H], F32)
-            for j in range(BLOCKS):
-                nc.tensor.transpose(back[:, j * P : (j + 1) * P], live["tanh_t", c][:, j, r * P : (r + 1) * P], ident[:])
-            live["back", i] = back
-
-        def store_tiles(view, held, c, r):
-            if c == CHUNKS - 1:
-                first = r
-            elif r == CHUNK - 1:
-                first = 0
-            else:
-                return
-            nc.sync.dma_start(out=view[:, c * CHUNK + first : c * CHUNK + r + 1, :], in_=held[:, first : r + 1, :])
-
-        def scale_m(i):
-            c, r = divmod(i, CHUNK)
-            if r == 0:
                 m_st = stores.tile([P, CHUNK, H], F32)
                 live["m", c] = m_st
-            nc.scalar.mul(live["m", c][:, r, :], live["back", i][:], M_SCALE)
-            store_tiles(m_v, live["m", c], c, r)
+            nc.scalar.mul(live["m", c][:, :, j * P : (j + 1) * P], live["back", b][:], M_SCALE)
+            store_blocks(m_v, live["m", c], c, j)
 
         def damp_cell(i):
             c, r = divmod(i, CHUNK)
-            damped = work.tile([P, H], F32, bufs=3)
-            nc.vector.tensor_tensor(out=damped[:], in0=live["c", c][:, r, :], in1=decay[:], op=MULT)
-            live["damped", i] = damped
-
-        def product(i):
-            c, r = divmod(i, CHUNK)
             if r == 0:
+                damped = work.tile([P, CHUNK, H], F32, bufs=3)
+                live["damped", c] = damped
+            nc.vector.tensor_tensor(out=live["damped", c][:, r, :], in0=live["c", c][:, r, :], in1=decay[:], op=MULT)
+
+        def product(b):
+            c, j = divmod(b, BLOCKS)
+            if j == 0:
                 i_st = stores.tile([P, CHUNK, H], F32)
                 live["i", c] = i_st
-            nc.vector.tensor_tensor(out=live["i", c][:, r, :], in0=live["m", c][:, r, :], in1=live["damped", i][:], op=MULT)
+            cols = slice(j * P, (j + 1) * P)
+            nc.vector.tensor_tensor(out=live["i", c][:, :, cols], in0=live["m", c][:, :, cols], in1=live["damped", c][:, :, cols], op=MULT)
 
-        def total(i):
-            c, r = divmod(i, CHUNK)
-            adder = nc.vector if c == CHUNKS - 1 else nc.gpsimd
-            adder.tensor_tensor(out=live["i", c][:, r, :], in0=live["i", c][:, r, :], in1=live["z", c][:, r, :], op=ADD)
-            store_tiles(i_v, live["i", c], c, r)
+        def total(b):
+            c, j = divmod(b, BLOCKS)
+            cols = slice(j * P, (j + 1) * P)
+            adder = nc.vector if c >= CHUNKS - VECTOR_SUMS else nc.gpsimd
+            adder.tensor_tensor(out=live["i", c][:, :, cols], in0=live["i", c][:, :, cols], in1=live["z", c][:, :, cols], op=ADD)
+            store_blocks(i_v, live["i", c], c, j)
 
         def run(stage, i):
             if 0 <= i < TILES:
@@ -312,6 +301,9 @@ def tile_koslmcell_pa_t_kernel(
             run(tanh_z, s - Z_TANH)
             run(regroup_tile, s)
             if s == 1:
+                nc.scalar.activation(out=decay_rows[0:1, :], in_=lam_row[:], func=ACT.Exp)
+            if s == 2:
                 spread_biases()
-            if s == 3:
                 spread_decay()
+            if s == 4:
+                turn_m_bias()

@@ -27,17 +27,19 @@ BLOCKS = H // P
 assert BLOCKS == CHUNK
 
 QUANTISE = 1
-Z_MULTIPLY = 2
-Z_BIAS = 3
-Z_TANH = 4
-M_MULTIPLY = 5
-M_TANH = 6
-TURN_BACK = 7
-M_OUT = 8
-PRODUCT = 9
-DAMP = 3
+LEAD = 4
+Z_MULTIPLY = 2 + LEAD
+Z_BIAS = 3 + LEAD
+Z_TANH = 4 + LEAD
+M_MULTIPLY = 5 + LEAD
+M_TANH = 6 + LEAD
+TURN_BACK = 7 + LEAD
+M_OUT = 8 + LEAD
+PRODUCT = 9 + LEAD
+DAMP = 3 + LEAD
 STEPS = TILES + PRODUCT
-VECTOR_SUMS = 2
+VECTOR_SUMS = 4
+FINE_STORES = 3
 
 FLOPS = 2 * BATCH * (2 * K) * (2 * H)
 
@@ -90,47 +92,80 @@ def tile_koslmcell_pa_t_kernel(
             nc.sync.dma_start(out=held[:], in_=view[:, c * CHUNK : (c + 1) * CHUNK, :])
             live[name, c] = held
 
-        load("x", x_v, 0)
-        load("h", h_v, 0)
-
+        ident = const.tile([P, P], F32)
+        make_identity(nc, ident[:])
+        ident_bf = const.tile([P, P], BF16)
+        make_identity(nc, ident_bf[:])
         words = {}
         planes = {}
-        for name, w_words in (("x", W_ih_words), ("h", W_hh_words)):
+        srcs = {"x": (W_ih_words, W_ih_scales), "h": (W_hh_words, W_hh_scales)}
+        for name in ("x", "h"):
             w_sb = const.tile([P, 4 * H], U8, name="words_" + name, align_bytes=64)
-            nc.sync.dma_start(out=w_sb[:].bitcast(I32), in_=w_words[0].bitcast(I32))
             words[name] = w_sb
-        for name, w_scales in (("x", W_ih_scales), ("h", W_hh_scales)):
             plane = const.tile([P, 2 * H], U8, name="plane_" + name, align_bytes=64)
             nc.vector.memset(plane[:].bitcast(I32), 0)
-            for quad in range(4):
-                nc.sync.dma_start(
-                    out=plane[32 * quad : 32 * quad + 4, :].bitcast(I32),
-                    in_=w_scales[0, 4 * quad : 4 * quad + 4, :].bitcast(I32),
-                )
             planes[name] = plane
-
         z_rows = const.tile([P, H], BF16)
         nc.vector.memset(z_rows[:].bitcast(I32), 0)
         m_rows = const.tile([P, P], BF16)
         nc.vector.memset(m_rows[:].bitcast(I32), 0)
         lam_row = const.tile([1, H], BF16)
-        nc.sync.dma_start(out=lam_row[:], in_=as_row(log_lambda))
-        nc.sync.dma_start(out=z_rows[0:1, :], in_=as_row(b_ih[0:H]))
-        nc.sync.dma_start(out=z_rows[1:2, :], in_=as_row(b_hh[0:H]))
-        nc.sync.dma_start(out=z_rows[2:3, :], in_=as_row(z_bias))
-        load("c", c_v, 0)
-        nc.sync.dma_start(out=m_rows[0:BLOCKS, :], in_=as_blocks(b_ih[H : 2 * H]))
-        nc.sync.dma_start(out=m_rows[BLOCKS : 2 * BLOCKS, :], in_=as_blocks(b_hh[H : 2 * H]))
-        nc.sync.dma_start(out=m_rows[2 * BLOCKS : 3 * BLOCKS, :], in_=as_blocks(m_bias))
-        for c in range(1, CHUNKS):
-            load("x", x_v, c)
-            load("h", h_v, c)
-            load("c", c_v, c)
 
-        ident = const.tile([P, P], F32)
-        make_identity(nc, ident[:])
-        ident_bf = const.tile([P, P], BF16)
-        make_identity(nc, ident_bf[:])
+        def load_words(name):
+            nc.sync.dma_start(out=words[name][:].bitcast(I32), in_=srcs[name][0][0].bitcast(I32))
+
+        def load_plane(name):
+            for quad in range(4):
+                nc.sync.dma_start(
+                    out=planes[name][32 * quad : 32 * quad + 4, :].bitcast(I32),
+                    in_=srcs[name][1][0, 4 * quad : 4 * quad + 4, :].bitcast(I32),
+                )
+
+        def load_lam():
+            nc.sync.dma_start(out=lam_row[:], in_=as_row(log_lambda))
+
+        def load_zb():
+            nc.sync.dma_start(out=z_rows[0:1, :], in_=as_row(b_ih[0:H]))
+            nc.sync.dma_start(out=z_rows[1:2, :], in_=as_row(b_hh[0:H]))
+            nc.sync.dma_start(out=z_rows[2:3, :], in_=as_row(z_bias))
+
+        def load_mb():
+            nc.sync.dma_start(out=m_rows[0:BLOCKS, :], in_=as_blocks(b_ih[H : 2 * H]))
+            nc.sync.dma_start(out=m_rows[BLOCKS : 2 * BLOCKS, :], in_=as_blocks(b_hh[H : 2 * H]))
+            nc.sync.dma_start(out=m_rows[2 * BLOCKS : 3 * BLOCKS, :], in_=as_blocks(m_bias))
+
+        load_lam()
+        load("x", x_v, 0)
+        load("h", h_v, 0)
+        load_plane("x")
+        load("x", x_v, 1)
+        load("h", h_v, 1)
+        load_plane("h")
+        load_words("x")
+        load_words("h")
+        load_zb()
+        load("x", x_v, 2)
+        load("h", h_v, 2)
+        load("c", c_v, 0)
+        load_mb()
+        load("x", x_v, 3)
+        load("h", h_v, 3)
+        load("c", c_v, 1)
+        load("c", c_v, 2)
+        load("c", c_v, 3)
+        load("x", x_v, 4)
+        load("h", h_v, 4)
+        load("c", c_v, 4)
+        load("x", x_v, 5)
+        load("h", h_v, 5)
+        load("c", c_v, 5)
+        load("x", x_v, 6)
+        load("h", h_v, 6)
+        load("c", c_v, 6)
+        load("x", x_v, 7)
+        load("h", h_v, 7)
+        load("c", c_v, 7)
+
         ones_bf = const.tile([P, P], BF16)
         nc.vector.memset(ones_bf[:], 1.0)
         ones = const.tile([P, P], F32)
@@ -175,8 +210,8 @@ def tile_koslmcell_pa_t_kernel(
         def quantise_tile(i):
             c, r = divmod(i, CHUNK)
             if r == 0:
-                codes = work.tile([P, 2, ROWS], U32, align_bytes=64)
-                scales = work.tile([P, 2, ROWS], U8, align_bytes=64)
+                codes = work.tile([P, 2, ROWS], U32, bufs=3, align_bytes=64)
+                scales = work.tile([P, 2, ROWS], U8, bufs=3, align_bytes=64)
                 live["codes", c] = codes
                 live["scales", c] = scales
             batch = slice(r * P, (r + 1) * P)
@@ -216,6 +251,9 @@ def tile_koslmcell_pa_t_kernel(
             nc.scalar.activation(out=live["z", c][:, r, :], in_=live["pre_z", i][:], func=ACT.Tanh)
             if c == CHUNKS - 1:
                 nc.sync.dma_start(out=z_v[:, i : i + 1, :], in_=live["z", c][:, r : r + 1, :])
+            elif c >= CHUNKS - FINE_STORES:
+                if r % 2 == 1:
+                    nc.sync.dma_start(out=z_v[:, i - 1 : i + 1, :], in_=live["z", c][:, r - 1 : r + 1, :])
             elif r == CHUNK - 1:
                 nc.sync.dma_start(out=z_v[:, c * CHUNK : (c + 1) * CHUNK, :], in_=live["z", c][:])
 
@@ -247,7 +285,7 @@ def tile_koslmcell_pa_t_kernel(
             live["back", b] = back
 
         def store_blocks(view, held, c, j):
-            width = BLOCKS // 2 if c == CHUNKS - 1 else BLOCKS
+            width = BLOCKS // 2 if c >= CHUNKS - FINE_STORES else BLOCKS
             if (j + 1) % width == 0:
                 cols = slice((j + 1 - width) * P, (j + 1) * P)
                 nc.sync.dma_start(out=view[:, c * CHUNK : (c + 1) * CHUNK, cols], in_=held[:, :, cols])
@@ -278,7 +316,7 @@ def tile_koslmcell_pa_t_kernel(
         def total(b):
             c, j = divmod(b, BLOCKS)
             cols = slice(j * P, (j + 1) * P)
-            adder = nc.vector if c >= CHUNKS - VECTOR_SUMS else nc.gpsimd
+            adder = nc.vector if b >= TILES - VECTOR_SUMS else nc.gpsimd
             adder.tensor_tensor(out=live["i", c][:, :, cols], in0=live["i", c][:, :, cols], in1=live["z", c][:, :, cols], op=ADD)
             store_blocks(i_v, live["i", c], c, j)
 
@@ -286,6 +324,7 @@ def tile_koslmcell_pa_t_kernel(
             if 0 <= i < TILES:
                 stage(i)
 
+        nc.scalar.activation(out=decay_rows[0:1, :], in_=lam_row[:], func=ACT.Exp)
         for s in range(STEPS):
             run(transpose_tile, s)
             run(turn_back, s - TURN_BACK)
@@ -300,10 +339,8 @@ def tile_koslmcell_pa_t_kernel(
             run(scale_m, s - M_OUT)
             run(tanh_z, s - Z_TANH)
             run(regroup_tile, s)
-            if s == 1:
-                nc.scalar.activation(out=decay_rows[0:1, :], in_=lam_row[:], func=ACT.Exp)
-            if s == 2:
+            if s == 2 + LEAD:
                 spread_biases()
                 spread_decay()
-            if s == 4:
+            if s == 4 + LEAD:
                 turn_m_bias()

@@ -26,7 +26,8 @@ CHUNKS = TILES // CHUNK
 BLOCKS = H // P
 assert BLOCKS == CHUNK
 
-QUANTISE = 1
+PAIR = 2
+QUANTISE = 2
 LEAD = 4
 Z_MULTIPLY = 2 + LEAD
 Z_BIAS = 3 + LEAD
@@ -35,7 +36,7 @@ M_MULTIPLY = 5 + LEAD
 M_TANH = 6 + LEAD
 TURN_BACK = 7 + LEAD
 M_OUT = 8 + LEAD
-PRODUCT = 9 + LEAD
+PRODUCT = 8 + LEAD
 DAMP = 3 + LEAD
 STEPS = TILES + PRODUCT
 VECTOR_SUMS = 4
@@ -203,24 +204,35 @@ def tile_koslmcell_pa_t_kernel(
             live["turned", i] = turned
 
         def regroup_tile(i):
-            grouped = work.tile([P, 2, P, 4], BF16, bufs=3, align_bytes=64)
-            nc.scalar.copy(out=grouped[:].bitcast(F32), in_=live["turned", i][:].rearrange("p a u r -> p a r u"))
-            live["grouped", i] = grouped
+            first, half = i - i % PAIR, i % PAIR
+            if half == 0:
+                grouped = work.tile([P, 2, PAIR * P, 4], BF16, bufs=2, align_bytes=64)
+                live["grouped", first] = grouped
+            copier = nc.vector.tensor_copy if i % 4 == 3 else nc.scalar.copy
+            copier(
+                out=live["grouped", first][:, :, half * P : (half + 1) * P, :].bitcast(F32),
+                in_=live["turned", i][:].rearrange("p a u r -> p a r u"),
+            )
 
-        def quantise_tile(i):
+        def quantise_tile(i, a):
             c, r = divmod(i, CHUNK)
-            if r == 0:
+            if r == 0 and a == 0:
                 codes = work.tile([P, 2, ROWS], U32, bufs=3, align_bytes=64)
                 scales = work.tile([P, 2, ROWS], U8, bufs=3, align_bytes=64)
                 live["codes", c] = codes
                 live["scales", c] = scales
-            batch = slice(r * P, (r + 1) * P)
-            for a in range(2):
-                nc.vector.quantize_mx(
-                    out=live["codes", c][:, a, batch].bitcast(FP8X4),
-                    scales=live["scales", c][:, a, batch],
-                    in_=live["grouped", i][:, a, :, :].rearrange("p r t -> p (r t)"),
-                )
+            batch = slice(r * P, (r + PAIR) * P)
+            nc.vector.quantize_mx(
+                out=live["codes", c][:, a, batch].bitcast(FP8X4),
+                scales=live["scales", c][:, a, batch],
+                in_=live["grouped", i][:, a, :, :].rearrange("p r t -> p (r t)"),
+            )
+
+        def quantise_x(i):
+            quantise_tile(i, 0)
+
+        def quantise_h(i):
+            quantise_tile(i, 1)
 
         def multiply_z(i):
             c, r = divmod(i, CHUNK)
@@ -303,7 +315,12 @@ def tile_koslmcell_pa_t_kernel(
             if r == 0:
                 damped = work.tile([P, CHUNK, H], F32, bufs=3)
                 live["damped", c] = damped
-            nc.vector.tensor_tensor(out=live["damped", c][:, r, :], in0=live["c", c][:, r, :], in1=decay[:], op=MULT)
+            nc.vector.tensor_tensor(
+                out=live["damped", c][:, r : r + PAIR, :],
+                in0=live["c", c][:, r : r + PAIR, :],
+                in1=decay[:].unsqueeze(1).to_broadcast([P, PAIR, H]),
+                op=MULT,
+            )
 
         def product(b):
             c, j = divmod(b, BLOCKS)
@@ -311,7 +328,7 @@ def tile_koslmcell_pa_t_kernel(
                 i_st = stores.tile([P, CHUNK, H], F32)
                 live["i", c] = i_st
             cols = slice(j * P, (j + 1) * P)
-            nc.vector.tensor_tensor(out=live["i", c][:, :, cols], in0=live["m", c][:, :, cols], in1=live["damped", c][:, :, cols], op=MULT)
+            nc.vector.scalar_tensor_tensor(out=live["i", c][:, :, cols], in0=live["back", b][:], scalar=M_SCALE, in1=live["damped", c][:, :, cols], op0=MULT, op1=MULT)
 
         def total(b):
             c, j = divmod(b, BLOCKS)
@@ -324,6 +341,10 @@ def tile_koslmcell_pa_t_kernel(
             if 0 <= i < TILES:
                 stage(i)
 
+        def run_pair(stage, i):
+            if i % PAIR == 0:
+                run(stage, i)
+
         nc.scalar.activation(out=decay_rows[0:1, :], in_=lam_row[:], func=ACT.Exp)
         for s in range(STEPS):
             run(transpose_tile, s)
@@ -332,13 +353,14 @@ def tile_koslmcell_pa_t_kernel(
             run(multiply_z, s - Z_MULTIPLY)
             run(product, s - PRODUCT)
             run(total, s - PRODUCT)
-            run(quantise_tile, s - QUANTISE)
+            run_pair(quantise_x, s - QUANTISE)
+            run_pair(quantise_h, s - QUANTISE - 1)
             run(add_bias_z, s - Z_BIAS)
-            run(damp_cell, s - DAMP)
+            run_pair(damp_cell, s - DAMP)
             run(tanh_m, s - M_TANH)
-            run(scale_m, s - M_OUT)
             run(tanh_z, s - Z_TANH)
             run(regroup_tile, s)
+            run(scale_m, s - M_OUT)
             if s == 2 + LEAD:
                 spread_biases()
                 spread_decay()

@@ -38,7 +38,7 @@ TURN_BACK = 7 + LEAD
 M_OUT = 8 + LEAD
 PRODUCT = 8 + LEAD
 DAMP = 3 + LEAD
-STEPS = TILES + PRODUCT
+STEPS = TILES + PRODUCT + 0
 VECTOR_SUMS = 4
 FINE_STORES = 3
 
@@ -325,7 +325,7 @@ def tile_koslmcell_pa_t_kernel(
         def product(b):
             c, j = divmod(b, BLOCKS)
             if j == 0:
-                i_st = stores.tile([P, CHUNK, H], F32)
+                i_st = stores.tile([P, CHUNK, H], F32, bufs=3)
                 live["i", c] = i_st
             cols = slice(j * P, (j + 1) * P)
             nc.vector.scalar_tensor_tensor(out=live["i", c][:, :, cols], in0=live["back", b][:], scalar=M_SCALE, in1=live["damped", c][:, :, cols], op0=MULT, op1=MULT)
@@ -335,6 +335,9 @@ def tile_koslmcell_pa_t_kernel(
             cols = slice(j * P, (j + 1) * P)
             adder = nc.vector if b >= TILES - VECTOR_SUMS else nc.gpsimd
             adder.tensor_tensor(out=live["i", c][:, :, cols], in0=live["i", c][:, :, cols], in1=live["z", c][:, :, cols], op=ADD)
+
+        def store_total(b):
+            c, j = divmod(b, BLOCKS)
             store_blocks(i_v, live["i", c], c, j)
 
         def run(stage, i):
@@ -361,6 +364,7 @@ def tile_koslmcell_pa_t_kernel(
             run(tanh_z, s - Z_TANH)
             run(regroup_tile, s)
             run(scale_m, s - M_OUT)
+            run(store_total, s - PRODUCT - 0)
             if s == 2 + LEAD:
                 spread_biases()
                 spread_decay()

@@ -88,10 +88,11 @@ def tile_koslmcell_pa_t_kernel(
 
         live = {}
 
-        def load(name, view, c):
+        def load(name, view, c, cuts=(0, CHUNK)):
             held = inputs.tile([P, CHUNK, K], BF16, name="%s%d" % (name, c))
-            nc.sync.dma_start(out=held[:], in_=view[:, c * CHUNK : (c + 1) * CHUNK, :])
             live[name, c] = held
+            for lo, hi in zip(cuts[:-1], cuts[1:]):
+                nc.sync.dma_start(out=held[:, lo:hi, :], in_=view[:, c * CHUNK + lo : c * CHUNK + hi, :])
 
         ident = const.tile([P, P], F32)
         make_identity(nc, ident[:])
@@ -136,8 +137,14 @@ def tile_koslmcell_pa_t_kernel(
             nc.sync.dma_start(out=m_rows[2 * BLOCKS : 3 * BLOCKS, :], in_=as_blocks(m_bias))
 
         load_lam()
-        load("x", x_v, 0)
-        load("h", h_v, 0)
+        first = {}
+        for name, view in (("x", x_v), ("h", h_v)):
+            held = inputs.tile([P, CHUNK, K], BF16, name="%s0" % name)
+            live[name, 0] = held
+            first[name] = view
+        for lo, hi in ((0, 1), (1, CHUNK)):
+            for name in ("x", "h"):
+                nc.sync.dma_start(out=live[name, 0][:, lo:hi, :], in_=first[name][:, lo:hi, :])
         load_plane("x")
         load("x", x_v, 1)
         load("h", h_v, 1)

@@ -26,54 +26,46 @@ CHUNKS = TILES // CHUNK
 BLOCKS = H // P
 assert BLOCKS == CHUNK
 
+
 PAIR = 2
+HALF = PAIR * P
 QUANTISE = 2
-LEAD = 4
-Z_MULTIPLY = 2 + LEAD
-Z_BIAS = 3 + LEAD
-Z_TANH = 4 + LEAD
-M_MULTIPLY = 5 + LEAD
-M_TANH = 6 + LEAD
-TURN_BACK = 7 + LEAD
-M_OUT = 8 + LEAD
-PRODUCT = 8 + LEAD
-DAMP = 3 + LEAD
-STEPS = TILES + PRODUCT + 0
+Z_MULTIPLY = 3
+Z_BIAS = 4
+Z_TANH = 5
+M_MULTIPLY = 6
+M_TANH = 7
+TURN_BACK = 8
+M_OUT = 9
+PRODUCT = 9
+DAMP = 5
+STEPS = TILES + 10
 VECTOR_SUMS = 4
-FINE_STORES = 3
+ZW = 4
+VREG = 4
+QH = 0
+STYLE = [4] * 8
+MSTORE = [4] * 8
+SETUP = 2
+ACCT = 1
+MBUF = 3
+IBUF = 3
+ORDER = "T qx qh su su2 B Mm Mz sm P tot tm bz tz dm rg st".split()
 
 FLOPS = 2 * BATCH * (2 * K) * (2 * H)
 
 
 def tile_koslmcell_pa_t_kernel(
-    tc,
-    x,
-    h_prev,
-    c_prev,
-    W_ih_words,
-    W_ih_scales,
-    b_ih,
-    W_hh_words,
-    W_hh_scales,
-    b_hh,
-    log_lambda,
-    z_bias,
-    m_bias,
-    out_0,
-    out_1,
-    out_2,
+    tc, x, h_prev, c_prev, W_ih_words, W_ih_scales, b_ih, W_hh_words, W_hh_scales, b_hh,
+    log_lambda, z_bias, m_bias, out_0, out_1, out_2,
 ):
     nc = tc.nc
-
     x_v = x.rearrange("(p t) k -> p t k", t=TILES)
     h_v = h_prev.rearrange("(p t) k -> p t k", t=TILES)
     c_v = c_prev.rearrange("(p t) k -> p t k", t=TILES)
     z_v = out_0.rearrange("(p t) k -> p t k", t=TILES)
     m_v = out_1.rearrange("(p t) k -> p t k", t=TILES)
     i_v = out_2.rearrange("(p t) k -> p t k", t=TILES)
-
-    def as_row(vector):
-        return vector.rearrange("(o n) -> o n", o=1)
 
     def as_blocks(vector):
         return vector.rearrange("(j p) -> j p", p=P)
@@ -87,12 +79,13 @@ def tile_koslmcell_pa_t_kernel(
         psum = ctx.enter_context(tc.psum_pool(name="psum", bufs=2))
 
         live = {}
+        views = {"x": x_v, "h": h_v, "c": c_v}
 
-        def load(name, view, c, cuts=(0, CHUNK)):
-            held = inputs.tile([P, CHUNK, K], BF16, name="%s%d" % (name, c))
-            live[name, c] = held
-            for lo, hi in zip(cuts[:-1], cuts[1:]):
-                nc.sync.dma_start(out=held[:, lo:hi, :], in_=view[:, c * CHUNK + lo : c * CHUNK + hi, :])
+        def load(name, c, lo=0, hi=CHUNK):
+            if (name, c) not in live:
+                held = inputs.tile([P, CHUNK, K], BF16, name="%s%d" % (name, c))
+                live[name, c] = held
+            nc.sync.dma_start(out=live[name, c][:, lo:hi, :], in_=views[name][:, c * CHUNK + lo : c * CHUNK + hi, :])
 
         ident = const.tile([P, P], F32)
         make_identity(nc, ident[:])
@@ -101,17 +94,18 @@ def tile_koslmcell_pa_t_kernel(
         words = {}
         planes = {}
         srcs = {"x": (W_ih_words, W_ih_scales), "h": (W_hh_words, W_hh_scales)}
+        spark = const.tile([P, 1], F32)
+        nc.vector.memset(spark[:], 0.0)
+        sparked = const.tile([P, 1], F32)
+        nc.scalar.activation(out=sparked[:], in_=spark[:], func=ACT.Tanh)
         for name in ("x", "h"):
             w_sb = const.tile([P, 4 * H], U8, name="words_" + name, align_bytes=64)
             words[name] = w_sb
             plane = const.tile([P, 2 * H], U8, name="plane_" + name, align_bytes=64)
             nc.vector.memset(plane[:].bitcast(I32), 0)
             planes[name] = plane
-        z_rows = const.tile([P, H], BF16)
-        nc.vector.memset(z_rows[:].bitcast(I32), 0)
-        m_rows = const.tile([P, P], BF16)
-        nc.vector.memset(m_rows[:].bitcast(I32), 0)
-        lam_row = const.tile([1, H], BF16)
+        rows = const.tile([P, P], BF16)
+        nc.vector.memset(rows[:].bitcast(I32), 0)
 
         def load_words(name):
             nc.sync.dma_start(out=words[name][:].bitcast(I32), in_=srcs[name][0][0].bitcast(I32))
@@ -123,83 +117,56 @@ def tile_koslmcell_pa_t_kernel(
                     in_=srcs[name][1][0, 4 * quad : 4 * quad + 4, :].bitcast(I32),
                 )
 
-        def load_lam():
-            nc.sync.dma_start(out=lam_row[:], in_=as_row(log_lambda))
+        def load_vectors():
+            nc.sync.dma_start(out=rows[0:8, :], in_=as_blocks(b_ih))
+            nc.sync.dma_start(out=rows[8:16, :], in_=as_blocks(b_hh))
+            nc.sync.dma_start(out=rows[16:20, :], in_=as_blocks(z_bias))
+            nc.sync.dma_start(out=rows[20:24, :], in_=as_blocks(m_bias))
+            nc.sync.dma_start(out=rows[24:28, :], in_=as_blocks(log_lambda))
 
-        def load_zb():
-            nc.sync.dma_start(out=z_rows[0:1, :], in_=as_row(b_ih[0:H]))
-            nc.sync.dma_start(out=z_rows[1:2, :], in_=as_row(b_hh[0:H]))
-            nc.sync.dma_start(out=z_rows[2:3, :], in_=as_row(z_bias))
-
-        def load_mb():
-            nc.sync.dma_start(out=m_rows[0:BLOCKS, :], in_=as_blocks(b_ih[H : 2 * H]))
-            nc.sync.dma_start(out=m_rows[BLOCKS : 2 * BLOCKS, :], in_=as_blocks(b_hh[H : 2 * H]))
-            nc.sync.dma_start(out=m_rows[2 * BLOCKS : 3 * BLOCKS, :], in_=as_blocks(m_bias))
-
-        load_lam()
-        first = {}
-        for name, view in (("x", x_v), ("h", h_v)):
-            held = inputs.tile([P, CHUNK, K], BF16, name="%s0" % name)
-            live[name, 0] = held
-            first[name] = view
-        for lo, hi in ((0, 1), (1, CHUNK)):
-            for name in ("x", "h"):
-                nc.sync.dma_start(out=live[name, 0][:, lo:hi, :], in_=first[name][:, lo:hi, :])
+        load("x", 0, 0, 1)
+        load("h", 0, 0, 1)
+        load("x", 0, 1, 4)
+        load("h", 0, 1, 4)
         load_plane("x")
-        load("x", x_v, 1)
-        load("h", h_v, 1)
-        load_plane("h")
         load_words("x")
+        load_plane("h")
         load_words("h")
-        load_zb()
-        load("x", x_v, 2)
-        load("h", h_v, 2)
-        load("c", c_v, 0)
-        load_mb()
-        load("x", x_v, 3)
-        load("h", h_v, 3)
-        load("c", c_v, 1)
-        load("c", c_v, 2)
-        load("c", c_v, 3)
-        load("x", x_v, 4)
-        load("h", h_v, 4)
-        load("c", c_v, 4)
-        load("x", x_v, 5)
-        load("h", h_v, 5)
-        load("c", c_v, 5)
-        load("x", x_v, 6)
-        load("h", h_v, 6)
-        load("c", c_v, 6)
-        load("x", x_v, 7)
-        load("h", h_v, 7)
-        load("c", c_v, 7)
-
-        ones_bf = const.tile([P, P], BF16)
-        nc.vector.memset(ones_bf[:], 1.0)
-        ones = const.tile([P, P], F32)
-        nc.vector.memset(ones[:], 1.0)
-        decay_rows = const.tile([P, H], F32)
-        nc.vector.memset(decay_rows[:].bitcast(I32), 0)
+        load_vectors()
+        load("x", 1)
+        load("h", 1)
+        load("c", 0)
+        for c in range(2, CHUNKS):
+            load("x", c)
+            load("h", c)
+            load("c", c - 1)
+        load("c", CHUNKS - 1)
 
         bias_z = const.tile([P, H], F32)
         bias_m = const.tile([P, BLOCKS], F32)
         decay = psum.tile([P, H], F32, bufs=1)
 
-        def spread_decay():
-            nc.tensor.matmul(out=decay[:], lhsT=ones[:], rhs=decay_rows[:], start=True, stop=True)
+        def set_up():
+            turned_rows = psum.tile([P, P], BF16, tag="back")
+            nc.tensor.transpose(turned_rows[:], rows[:], ident_bf[:])
+            cols = const.tile([P, 28], F32)
+            nc.vector.tensor_copy(out=cols[:], in_=turned_rows[:, 0:28])
+            both = const.tile([P, 8], F32)
+            nc.vector.tensor_tensor(out=both[:], in0=cols[:, 0:8], in1=cols[:, 8:16], op=ADD)
+            sums = const.tile([P, 8], F32)
+            nc.vector.tensor_tensor(out=sums[:], in0=both[:], in1=cols[:, 16:24], op=ADD)
+            lam = const.tile([P, BLOCKS], F32)
+            nc.scalar.activation(out=lam[:], in_=cols[:, 24:28], func=ACT.Exp)
+            live["sums"] = sums
+            live["lam"] = lam
 
-        def spread_biases():
+        def set_up_2():
             z_spread = psum.tile([P, H], F32, tag="acc_z")
-            nc.tensor.matmul(out=z_spread[:], lhsT=ones_bf[:], rhs=z_rows[:], start=True, stop=True)
+            for j in range(BLOCKS):
+                nc.tensor.transpose(z_spread[:, j * P : (j + 1) * P], live["sums"][:, j : j + 1].to_broadcast([P, P]), ident[:])
             nc.vector.tensor_copy(out=bias_z[:], in_=z_spread[:])
-
-        def turn_m_bias():
-            m_turned = psum.tile([P, P], BF16, tag="back")
-            nc.tensor.transpose(m_turned[:], m_rows[:], ident_bf[:])
-            m_cols = const.tile([P, 3 * BLOCKS], F32)
-            nc.vector.tensor_copy(out=m_cols[:], in_=m_turned[:, 0 : 3 * BLOCKS])
-            nc.vector.tensor_tensor(out=bias_m[:], in0=m_cols[:, 0:BLOCKS], in1=m_cols[:, BLOCKS : 2 * BLOCKS], op=ADD)
-            nc.vector.tensor_tensor(out=bias_m[:], in0=bias_m[:], in1=m_cols[:, 2 * BLOCKS : 3 * BLOCKS], op=ADD)
+            for j in range(BLOCKS):
+                nc.tensor.transpose(decay[:, j * P : (j + 1) * P], live["lam"][:, j : j + 1].to_broadcast([P, P]), ident[:])
 
         def transpose_tile(i):
             c, r = divmod(i, CHUNK)
@@ -215,7 +182,7 @@ def tile_koslmcell_pa_t_kernel(
             if half == 0:
                 grouped = work.tile([P, 2, PAIR * P, 4], BF16, bufs=2, align_bytes=64)
                 live["grouped", first] = grouped
-            copier = nc.vector.tensor_copy if i % 4 == 3 else nc.scalar.copy
+            copier = nc.vector.tensor_copy if i % VREG == VREG - 1 else nc.scalar.copy
             copier(
                 out=live["grouped", first][:, :, half * P : (half + 1) * P, :].bitcast(F32),
                 in_=live["turned", i][:].rearrange("p a u r -> p a r u"),
@@ -223,7 +190,7 @@ def tile_koslmcell_pa_t_kernel(
 
         def quantise_tile(i, a):
             c, r = divmod(i, CHUNK)
-            if r == 0 and a == 0:
+            if a == 0 and r == 0:
                 codes = work.tile([P, 2, ROWS], U32, bufs=3, align_bytes=64)
                 scales = work.tile([P, 2, ROWS], U8, bufs=3, align_bytes=64)
                 live["codes", c] = codes
@@ -268,54 +235,76 @@ def tile_koslmcell_pa_t_kernel(
                 z_st = stores.tile([P, CHUNK, H], F32, bufs=3)
                 live["z", c] = z_st
             nc.scalar.activation(out=live["z", c][:, r, :], in_=live["pre_z", i][:], func=ACT.Tanh)
-            if c == CHUNKS - 1:
-                nc.sync.dma_start(out=z_v[:, i : i + 1, :], in_=live["z", c][:, r : r + 1, :])
-            elif c >= CHUNKS - FINE_STORES:
-                if r % 2 == 1:
-                    nc.sync.dma_start(out=z_v[:, i - 1 : i + 1, :], in_=live["z", c][:, r - 1 : r + 1, :])
-            elif r == CHUNK - 1:
-                nc.sync.dma_start(out=z_v[:, c * CHUNK : (c + 1) * CHUNK, :], in_=live["z", c][:])
+            w = 1 if c == CHUNKS - 1 else ZW
+            if (r + 1) % w == 0:
+                nc.sync.dma_start(out=z_v[:, i + 1 - w : i + 1, :], in_=live["z", c][:, r + 1 - w : r + 1, :])
+
+        def unit(b):
+            c, k = divmod(b, CHUNK)
+            n = STYLE[c]
+            if n == 4:
+                return c, 0, 4, k, 1
+            return c, 2 * (k // 2), 2, 2 * (k % 2), 2
 
         def multiply_m(b):
-            c, j = divmod(b, BLOCKS)
-            acc_t = psum.tile([P, ROWS], F32, bufs=1)
-            for a, name in enumerate(("x", "h")):
-                nc.tensor.matmul_mx(
-                    out=acc_t[:],
-                    lhsT=words[name][:, 2 * (H + j * P) : 2 * (H + (j + 1) * P)].bitcast(FP4X4),
-                    lhsT_scale=planes[name][:, H + j * P : H + (j + 1) * P],
-                    rhs=live["codes", c][:, a, :].bitcast(FP8X4),
-                    rhs_scale=live["scales", c][:, a, :],
-                    start=(a == 0),
-                    stop=(a == 1),
-                )
+            c, r0, nr, j0, nj = unit(b)
+            acc_t = psum.tile([P, nj, nr * P], F32, bufs=ACCT)
+            step = nr * P if nr == 4 else P
+            for v in range(nj):
+                j = j0 + v
+                for lo in range(0, nr * P, step):
+                    for a, name in enumerate(("x", "h")):
+                        cols = slice(r0 * P + lo, r0 * P + lo + step)
+                        nc.tensor.matmul_mx(
+                            out=acc_t[:, v, lo : lo + step],
+                            lhsT=words[name][:, 2 * (H + j * P) : 2 * (H + (j + 1) * P)].bitcast(FP4X4),
+                            lhsT_scale=planes[name][:, H + j * P : H + (j + 1) * P],
+                            rhs=live["codes", c][:, a, cols].bitcast(FP8X4),
+                            rhs_scale=live["scales", c][:, a, cols],
+                            start=(a == 0),
+                            stop=(a == 1),
+                        )
             live["acc_t", b] = acc_t
 
         def tanh_m(b):
-            j = b % BLOCKS
-            tanh_t = work.tile([P, ROWS], F32, bufs=3)
-            nc.scalar.activation(out=tanh_t[:], in_=live["acc_t", b][:], func=ACT.Tanh, bias=bias_m[:, j : j + 1])
+            c, r0, nr, j0, nj = unit(b)
+            tanh_t = work.tile([P, nj, nr * P], F32, bufs=3)
+            for v in range(nj):
+                j = j0 + v
+                nc.scalar.activation(out=tanh_t[:, v, :], in_=live["acc_t", b][:, v, :], func=ACT.Tanh, bias=live["sums"][:, BLOCKS + j : BLOCKS + j + 1])
             live["tanh_t", b] = tanh_t
 
         def turn_back(b):
-            back = psum.tile([P, CHUNK, P], F32)
-            for r in range(CHUNK):
-                nc.tensor.transpose(back[:, r, :], live["tanh_t", b][:, r * P : (r + 1) * P], ident[:])
+            c, r0, nr, j0, nj = unit(b)
+            back = psum.tile([P, nr, nj, P], F32)
+            for r in range(nr):
+                for v in range(nj):
+                    nc.tensor.transpose(back[:, r, v, :], live["tanh_t", b][:, v, r * P : (r + 1) * P], ident[:])
             live["back", b] = back
 
-        def store_blocks(view, held, c, j):
-            width = BLOCKS // 2 if c >= CHUNKS - FINE_STORES else BLOCKS
-            if (j + 1) % width == 0:
-                cols = slice((j + 1 - width) * P, (j + 1) * P)
-                nc.sync.dma_start(out=view[:, c * CHUNK : (c + 1) * CHUNK, cols], in_=held[:, :, cols])
+        def area(b):
+            c, r0, nr, j0, nj = unit(b)
+            return slice(r0, r0 + nr), slice(j0 * P, (j0 + nj) * P)
+
+        def store_unit(view, held, b):
+            c, r0, nr, j0, nj = unit(b)
+            if nr == 2:
+                if j0 == 2:
+                    nc.sync.dma_start(out=view[:, c * CHUNK + r0 : c * CHUNK + r0 + 2, :], in_=held[:, r0 : r0 + 2, :])
+            else:
+                w = MSTORE[c]
+                if (j0 + 1) % w == 0:
+                    cols = slice((j0 + 1 - w) * P, (j0 + 1) * P)
+                    nc.sync.dma_start(out=view[:, c * CHUNK : (c + 1) * CHUNK, cols], in_=held[:, :, cols])
 
         def scale_m(b):
-            c, j = divmod(b, BLOCKS)
-            if j == 0:
-                m_st = stores.tile([P, CHUNK, H], F32)
+            c, k = divmod(b, CHUNK)
+            if k == 0:
+                m_st = stores.tile([P, CHUNK, H], F32, bufs=MBUF)
                 live["m", c] = m_st
-            nc.scalar.mul(live["m", c][:, :, j * P : (j + 1) * P], live["back", b][:], M_SCALE)
-            store_blocks(m_v, live["m", c], c, j)
+            rs, cs = area(b)
+            nc.scalar.mul(live["m", c][:, rs, cs], live["back", b][:].rearrange("p r v n -> p r (v n)"), M_SCALE)
+            store_unit(m_v, live["m", c], b)
 
         def damp_cell(i):
             c, r = divmod(i, CHUNK)
@@ -330,22 +319,21 @@ def tile_koslmcell_pa_t_kernel(
             )
 
         def product(b):
-            c, j = divmod(b, BLOCKS)
-            if j == 0:
-                i_st = stores.tile([P, CHUNK, H], F32, bufs=3)
+            c, k = divmod(b, CHUNK)
+            if k == 0:
+                i_st = stores.tile([P, CHUNK, H], F32, bufs=IBUF)
                 live["i", c] = i_st
-            cols = slice(j * P, (j + 1) * P)
-            nc.vector.scalar_tensor_tensor(out=live["i", c][:, :, cols], in0=live["back", b][:], scalar=M_SCALE, in1=live["damped", c][:, :, cols], op0=MULT, op1=MULT)
+            rs, cs = area(b)
+            nc.vector.scalar_tensor_tensor(out=live["i", c][:, rs, cs], in0=live["back", b][:].rearrange("p r v n -> p r (v n)"), scalar=M_SCALE, in1=live["damped", c][:, rs, cs], op0=MULT, op1=MULT)
 
         def total(b):
-            c, j = divmod(b, BLOCKS)
-            cols = slice(j * P, (j + 1) * P)
+            c, k = divmod(b, CHUNK)
+            rs, cs = area(b)
             adder = nc.vector if b >= TILES - VECTOR_SUMS else nc.gpsimd
-            adder.tensor_tensor(out=live["i", c][:, :, cols], in0=live["i", c][:, :, cols], in1=live["z", c][:, :, cols], op=ADD)
+            adder.tensor_tensor(out=live["i", c][:, rs, cs], in0=live["i", c][:, rs, cs], in1=live["z", c][:, rs, cs], op=ADD)
 
         def store_total(b):
-            c, j = divmod(b, BLOCKS)
-            store_blocks(i_v, live["i", c], c, j)
+            store_unit(i_v, live["i", b // CHUNK], b)
 
         def run(stage, i):
             if 0 <= i < TILES:
@@ -355,25 +343,25 @@ def tile_koslmcell_pa_t_kernel(
             if i % PAIR == 0:
                 run(stage, i)
 
-        nc.scalar.activation(out=decay_rows[0:1, :], in_=lam_row[:], func=ACT.Exp)
+        stages = {
+            "T": lambda s: run(transpose_tile, s),
+            "B": lambda s: run(turn_back, s - TURN_BACK),
+            "Mm": lambda s: run(multiply_m, s - M_MULTIPLY),
+            "Mz": lambda s: run(multiply_z, s - Z_MULTIPLY),
+            "P": lambda s: run(product, s - PRODUCT),
+            "tot": lambda s: run(total, s - PRODUCT),
+            "qx": lambda s: run_pair(quantise_x, s - QUANTISE),
+            "qh": lambda s: run_pair(quantise_h, s - QUANTISE - QH),
+            "bz": lambda s: run(add_bias_z, s - Z_BIAS),
+            "dm": lambda s: run_pair(damp_cell, s - DAMP),
+            "tm": lambda s: run(tanh_m, s - M_TANH),
+            "tz": lambda s: run(tanh_z, s - Z_TANH),
+            "rg": lambda s: run(regroup_tile, s),
+            "sm": lambda s: run(scale_m, s - M_OUT),
+            "st": lambda s: run(store_total, s - PRODUCT),
+            "su": lambda s: set_up() if s == SETUP else None,
+            "su2": lambda s: set_up_2() if s == SETUP + 1 else None,
+        }
         for s in range(STEPS):
-            run(transpose_tile, s)
-            run(turn_back, s - TURN_BACK)
-            run(multiply_m, s - M_MULTIPLY)
-            run(multiply_z, s - Z_MULTIPLY)
-            run(product, s - PRODUCT)
-            run(total, s - PRODUCT)
-            run_pair(quantise_x, s - QUANTISE)
-            run_pair(quantise_h, s - QUANTISE - 1)
-            run(add_bias_z, s - Z_BIAS)
-            run_pair(damp_cell, s - DAMP)
-            run(tanh_m, s - M_TANH)
-            run(tanh_z, s - Z_TANH)
-            run(regroup_tile, s)
-            run(scale_m, s - M_OUT)
-            run(store_total, s - PRODUCT - 0)
-            if s == 2 + LEAD:
-                spread_biases()
-                spread_decay()
-            if s == 4 + LEAD:
-                turn_m_bias()
+            for name in ORDER:
+                stages[name](s)

@@ -30,27 +30,43 @@ assert BLOCKS == CHUNK
 PAIR = 2
 HALF = PAIR * P
 QUANTISE = 2
-Z_MULTIPLY = 3
-Z_BIAS = 4
-Z_TANH = 5
-M_MULTIPLY = 6
-M_TANH = 7
-TURN_BACK = 8
-M_OUT = 9
-PRODUCT = 9
+Z_MULTIPLY = 5
+Z_BIAS = 6
+Z_TANH = 8
+M_MULTIPLY = 7
+M_TANH = 8
+TURN_BACK = 9
+M_OUT = 10
+PRODUCT = 10
 DAMP = 5
-STEPS = TILES + 10
+TOT = 11
+STEPS = TILES + 12
 VECTOR_SUMS = 4
 ZW = 4
-VREG = 4
+VREG = (3,)
+QLAG = 1
+QSPLIT = 2
+GD = ()
+DC = 4
+TZ = 2
+XB = 6
+QPAIRS = (0,)
+RGL = 0
+VREG0 = (1, 3)
+WARM = 0
+WARM2 = 0
+GPV = 1
+LOADS = "xt0 ht0 xr hr px x1 h1 wx wh ph x2 h2 c0".split()
 QH = 0
 STYLE = [4] * 8
 MSTORE = [4] * 8
-SETUP = 2
+SETUP = 4
+SETUP2 = 5
 ACCT = 1
-MBUF = 3
+MBUF = 2
 IBUF = 3
-ORDER = "T qx qh su su2 B Mm Mz sm P tot tm bz tz dm rg st".split()
+DBUF = 2
+ORDER = "T su su2 B Mm Mz sm P tot qx qh tm bz tz dm rg st".split()
 
 FLOPS = 2 * BATCH * (2 * K) * (2 * H)
 
@@ -83,14 +99,22 @@ def tile_koslmcell_pa_t_kernel(
 
         def load(name, c, lo=0, hi=CHUNK):
             if (name, c) not in live:
-                held = inputs.tile([P, CHUNK, K], BF16, name="%s%d" % (name, c))
+                held = inputs.tile([P, CHUNK, K], BF16, name="in_" + name, bufs=XB)
                 live[name, c] = held
             nc.sync.dma_start(out=live[name, c][:, lo:hi, :], in_=views[name][:, c * CHUNK + lo : c * CHUNK + hi, :])
 
         ident = const.tile([P, P], F32)
         make_identity(nc, ident[:])
+        warm_in = const.tile([P, 512], BF16)
+        nc.vector.memset(warm_in[:].bitcast(I32), 0)
+
+        def warm(n):
+            if n:
+                warm_out = psum.tile([P, H], F32, tag="acc_z")
+                for v in range(n):
+                    nc.tensor.matmul(out=warm_out[:], lhsT=warm_in[:, 0:P], rhs=warm_in[:], start=True, stop=True)
+
         ident_bf = const.tile([P, P], BF16)
-        make_identity(nc, ident_bf[:])
         words = {}
         planes = {}
         srcs = {"x": (W_ih_words, W_ih_scales), "h": (W_hh_words, W_hh_scales)}
@@ -118,28 +142,36 @@ def tile_koslmcell_pa_t_kernel(
                 )
 
         def load_vectors():
-            nc.sync.dma_start(out=rows[0:8, :], in_=as_blocks(b_ih))
-            nc.sync.dma_start(out=rows[8:16, :], in_=as_blocks(b_hh))
-            nc.sync.dma_start(out=rows[16:20, :], in_=as_blocks(z_bias))
-            nc.sync.dma_start(out=rows[20:24, :], in_=as_blocks(m_bias))
-            nc.sync.dma_start(out=rows[24:28, :], in_=as_blocks(log_lambda))
+            q = nc.gpsimd if GPV else nc.sync
+            q.dma_start(out=rows[0:8, :], in_=as_blocks(b_ih))
+            q.dma_start(out=rows[8:16, :], in_=as_blocks(b_hh))
+            q.dma_start(out=rows[16:20, :], in_=as_blocks(z_bias))
+            q.dma_start(out=rows[20:24, :], in_=as_blocks(m_bias))
+            q.dma_start(out=rows[24:28, :], in_=as_blocks(log_lambda))
 
-        load("x", 0, 0, 1)
-        load("h", 0, 0, 1)
-        load("x", 0, 1, 4)
-        load("h", 0, 1, 4)
-        load_plane("x")
-        load_words("x")
-        load_plane("h")
-        load_words("h")
-        load_vectors()
-        load("x", 1)
-        load("h", 1)
-        load("c", 0)
+        if GPV:
+            load_vectors()
+        make_identity(nc, ident_bf[:])
+        table = {
+            "xt0": lambda: load("x", 0, 0, 1), "ht0": lambda: load("h", 0, 0, 1),
+            "xr": lambda: load("x", 0, 1, 4), "hr": lambda: load("h", 0, 1, 4),
+            "x0": lambda: load("x", 0), "h0": lambda: load("h", 0),
+            "xa": lambda: load("x", 0, 0, 2), "ha": lambda: load("h", 0, 0, 2),
+            "xb": lambda: load("x", 0, 2, 4), "hb": lambda: load("h", 0, 2, 4),
+            "px": lambda: load_plane("x"), "ph": lambda: load_plane("h"),
+            "wx": lambda: load_words("x"), "wh": lambda: load_words("h"),
+            "vec": lambda: None if GPV else load_vectors(),
+        }
+        for name in LOADS:
+            if name in table:
+                table[name]()
+            else:
+                load(name[0], int(name[1]))
         for c in range(2, CHUNKS):
-            load("x", c)
-            load("h", c)
-            load("c", c - 1)
+            for name in ("x", "h", "c"):
+                k = c if name != "c" else c - 1
+                if (name, k) not in live:
+                    load(name, k)
         load("c", CHUNKS - 1)
 
         bias_z = const.tile([P, H], F32)
@@ -167,6 +199,10 @@ def tile_koslmcell_pa_t_kernel(
             nc.vector.tensor_copy(out=bias_z[:], in_=z_spread[:])
             for j in range(BLOCKS):
                 nc.tensor.transpose(decay[:, j * P : (j + 1) * P], live["lam"][:, j : j + 1].to_broadcast([P, P]), ident[:])
+            if GD:
+                decay_sb = const.tile([P, H], F32)
+                nc.vector.tensor_copy(out=decay_sb[:], in_=decay[:])
+                live["decay_sb"] = decay_sb
 
         def transpose_tile(i):
             c, r = divmod(i, CHUNK)
@@ -178,35 +214,47 @@ def tile_koslmcell_pa_t_kernel(
             live["turned", i] = turned
 
         def regroup_tile(i):
-            first, half = i - i % PAIR, i % PAIR
-            if half == 0:
-                grouped = work.tile([P, 2, PAIR * P, 4], BF16, bufs=2, align_bytes=64)
-                live["grouped", first] = grouped
-            copier = nc.vector.tensor_copy if i % VREG == VREG - 1 else nc.scalar.copy
+            c, r = divmod(i, CHUNK)
+            if r == 0:
+                grouped = work.tile([P, 2, ROWS, 4], BF16, bufs=2, align_bytes=64)
+                live["grouped", c] = grouped
+            copier = nc.vector.tensor_copy if r in (VREG0 if c == 0 else VREG) else nc.scalar.copy
             copier(
-                out=live["grouped", first][:, :, half * P : (half + 1) * P, :].bitcast(F32),
+                out=live["grouped", c][:, :, r * P : (r + 1) * P, :].bitcast(F32),
                 in_=live["turned", i][:].rearrange("p a u r -> p a r u"),
             )
 
-        def quantise_tile(i, a):
-            c, r = divmod(i, CHUNK)
-            if a == 0 and r == 0:
+        def quantise(c, a0, a1, lo, hi):
+            if ("codes", c) not in live:
                 codes = work.tile([P, 2, ROWS], U32, bufs=3, align_bytes=64)
                 scales = work.tile([P, 2, ROWS], U8, bufs=3, align_bytes=64)
                 live["codes", c] = codes
                 live["scales", c] = scales
-            batch = slice(r * P, (r + PAIR) * P)
-            nc.vector.quantize_mx(
-                out=live["codes", c][:, a, batch].bitcast(FP8X4),
-                scales=live["scales", c][:, a, batch],
-                in_=live["grouped", i][:, a, :, :].rearrange("p r t -> p (r t)"),
-            )
+            if a1 - a0 == 2:
+                nc.vector.quantize_mx(
+                    out=live["codes", c][:].rearrange("p a r -> p (a r)").bitcast(FP8X4),
+                    scales=live["scales", c][:].rearrange("p a r -> p (a r)"),
+                    in_=live["grouped", c][:].rearrange("p a r t -> p (a r t)"),
+                )
+            else:
+                nc.vector.quantize_mx(
+                    out=live["codes", c][:, a0, lo:hi].bitcast(FP8X4),
+                    scales=live["scales", c][:, a0, lo:hi],
+                    in_=live["grouped", c][:, a0, lo:hi, :].rearrange("p r t -> p (r t)"),
+                )
 
-        def quantise_x(i):
-            quantise_tile(i, 0)
-
-        def quantise_h(i):
-            quantise_tile(i, 1)
+        def quantise_step(s, part):
+            c, r = divmod(s, CHUNK)
+            if not 0 <= c < CHUNKS:
+                return
+            if c in QPAIRS:
+                if r % 2 == 1:
+                    quantise(c, part, part + 1, (r - 1) * P, (r + 1) * P)
+            elif r == 3:
+                if QSPLIT == 2:
+                    quantise(c, part, part + 1, 0, ROWS)
+                elif part == 0:
+                    quantise(c, 0, 2, 0, ROWS)
 
         def multiply_z(i):
             c, r = divmod(i, CHUNK)
@@ -225,19 +273,23 @@ def tile_koslmcell_pa_t_kernel(
             live["acc_z", i] = acc_z
 
         def add_bias_z(i):
-            pre_z = work.tile([P, H], F32, bufs=3)
-            nc.vector.tensor_tensor(out=pre_z[:], in0=live["acc_z", i][:], in1=bias_z[:], op=ADD)
-            live["pre_z", i] = pre_z
+            g = i % TZ
+            if g == 0:
+                pre_z = work.tile([P, TZ, H], F32, bufs=3)
+                live["pre_z", i] = pre_z
+            nc.vector.tensor_tensor(out=live["pre_z", i - g][:, g, :], in0=live["acc_z", i][:], in1=bias_z[:], op=ADD)
 
         def tanh_z(i):
             c, r = divmod(i, CHUNK)
             if r == 0:
                 z_st = stores.tile([P, CHUNK, H], F32, bufs=3)
                 live["z", c] = z_st
-            nc.scalar.activation(out=live["z", c][:, r, :], in_=live["pre_z", i][:], func=ACT.Tanh)
-            w = 1 if c == CHUNKS - 1 else ZW
-            if (r + 1) % w == 0:
-                nc.sync.dma_start(out=z_v[:, i + 1 - w : i + 1, :], in_=live["z", c][:, r + 1 - w : r + 1, :])
+            if i % TZ == 0:
+                nc.scalar.activation(out=live["z", c][:, r : r + TZ, :], in_=live["pre_z", i][:], func=ACT.Tanh)
+                w = min(ZW, 2) if c == CHUNKS - 1 else ZW
+                e = r + TZ
+                if e % w == 0:
+                    nc.sync.dma_start(out=z_v[:, c * CHUNK + e - w : c * CHUNK + e, :], in_=live["z", c][:, e - w : e, :])
 
         def unit(b):
             c, k = divmod(b, CHUNK)
@@ -309,14 +361,20 @@ def tile_koslmcell_pa_t_kernel(
         def damp_cell(i):
             c, r = divmod(i, CHUNK)
             if r == 0:
-                damped = work.tile([P, CHUNK, H], F32, bufs=3)
+                damped = work.tile([P, CHUNK, H], F32, bufs=DBUF)
                 live["damped", c] = damped
-            nc.vector.tensor_tensor(
-                out=live["damped", c][:, r : r + PAIR, :],
-                in0=live["c", c][:, r : r + PAIR, :],
-                in1=decay[:].unsqueeze(1).to_broadcast([P, PAIR, H]),
-                op=MULT,
-            )
+            if r in GD:
+                nc.gpsimd.tensor_tensor(out=live["damped", c][:, r, :], in0=live["c", c][:, r, :], in1=live["decay_sb"][:], op=MULT)
+            elif (r % DC == 0) or ((r - 1) in GD):
+                n = DC
+                while any((r + v) in GD or r + v >= CHUNK for v in range(n)):
+                    n -= 1
+                nc.vector.tensor_tensor(
+                    out=live["damped", c][:, r : r + n, :],
+                    in0=live["c", c][:, r : r + n, :],
+                    in1=decay[:].unsqueeze(1).to_broadcast([P, n, H]),
+                    op=MULT,
+                )
 
         def product(b):
             c, k = divmod(b, CHUNK)
@@ -349,19 +407,22 @@ def tile_koslmcell_pa_t_kernel(
             "Mm": lambda s: run(multiply_m, s - M_MULTIPLY),
             "Mz": lambda s: run(multiply_z, s - Z_MULTIPLY),
             "P": lambda s: run(product, s - PRODUCT),
-            "tot": lambda s: run(total, s - PRODUCT),
-            "qx": lambda s: run_pair(quantise_x, s - QUANTISE),
-            "qh": lambda s: run_pair(quantise_h, s - QUANTISE - QH),
+            "tot": lambda s: run(total, s - TOT),
+            "qx": lambda s: quantise_step(s - QLAG, 0),
+            "qh": lambda s: quantise_step(s - QLAG, 1),
             "bz": lambda s: run(add_bias_z, s - Z_BIAS),
-            "dm": lambda s: run_pair(damp_cell, s - DAMP),
+            "dm": lambda s: run(damp_cell, s - DAMP),
             "tm": lambda s: run(tanh_m, s - M_TANH),
             "tz": lambda s: run(tanh_z, s - Z_TANH),
-            "rg": lambda s: run(regroup_tile, s),
+            "rg": lambda s: run(regroup_tile, s - RGL),
             "sm": lambda s: run(scale_m, s - M_OUT),
-            "st": lambda s: run(store_total, s - PRODUCT),
+            "st": lambda s: run(store_total, s - TOT),
             "su": lambda s: set_up() if s == SETUP else None,
-            "su2": lambda s: set_up_2() if s == SETUP + 1 else None,
+            "su2": lambda s: set_up_2() if s == SETUP2 else None,
         }
+        warm(WARM)
         for s in range(STEPS):
+            if 0 < s < 5:
+                warm(WARM2)
             for name in ORDER:
                 stages[name](s)

@@ -55,8 +55,8 @@ RGL = 0
 VREG0 = (1, 3)
 WARM = 0
 WARM2 = 0
-GPV = 1
-LOADS = "xt0 ht0 xr hr px x1 h1 wx wh ph x2 h2 c0".split()
+GPV = 0
+LOADS = "xt0 ht0 xr hr vec x1 h1 px wx wh ph x2 h2 c0".split()
 QH = 0
 STYLE = [4] * 8
 MSTORE = [4] * 8

@@ -32,7 +32,7 @@ HALF = PAIR * P
 QUANTISE = 2
 Z_MULTIPLY = 5
 Z_BIAS = 6
-Z_TANH = 8
+Z_TANH = 7
 M_MULTIPLY = 7
 M_TANH = 8
 TURN_BACK = 9
@@ -48,7 +48,7 @@ QLAG = 1
 QSPLIT = 2
 GD = ()
 DC = 4
-TZ = 2
+TZ = 1
 XB = 6
 QPAIRS = (0,)
 RGL = 0

@@ -33,21 +33,21 @@ QUANTISE = 2
 Z_MULTIPLY = 5
 Z_BIAS = 6
 Z_TANH = 7
-M_MULTIPLY = 7
-M_TANH = 8
-TURN_BACK = 9
-M_OUT = 10
-PRODUCT = 10
-DAMP = 5
-TOT = 11
-STEPS = TILES + 12
-VECTOR_SUMS = 4
+M_MULTIPLY = 8
+M_TANH = 9
+TURN_BACK = 10
+M_OUT = 11
+PRODUCT = 11
+DAMP = 6
+TOT = 12
+STEPS = TILES + 13
+VECTOR_SUMS = 2
 ZW = 4
 VREG = (3,)
 QLAG = 1
 QSPLIT = 2
-GD = ()
-DC = 4
+GD = (2,)
+DC = 2
 TZ = 1
 XB = 6
 QPAIRS = (0,)
@@ -60,13 +60,17 @@ LOADS = "xt0 ht0 xr hr vec x1 h1 px wx wh ph x2 h2 c0".split()
 QH = 0
 STYLE = [4] * 8
 MSTORE = [4] * 8
-SETUP = 4
-SETUP2 = 5
+SETUP = 3
+SETUP2 = 4
+DSB = 1
 ACCT = 1
+BANKS = 7
+ACCZ = 2
+DPS = 1
 MBUF = 2
 IBUF = 3
 DBUF = 2
-ORDER = "T su su2 B Mm Mz sm P tot qx qh tm bz tz dm rg st".split()
+ORDER = "T sm P B su Mm Mz tm bz qx qh tz dm su2 rg tot st".split()
 
 FLOPS = 2 * BATCH * (2 * K) * (2 * H)
 
@@ -95,6 +99,9 @@ def tile_koslmcell_pa_t_kernel(
         psum = ctx.enter_context(tc.psum_pool(name="psum", bufs=2))
 
         live = {}
+
+        def bank(tag, bufs):
+            return {"tag": "bank", "bufs": BANKS} if BANKS else {"tag": tag, "bufs": bufs}
         views = {"x": x_v, "h": h_v, "c": c_v}
 
         def load(name, c, lo=0, hi=CHUNK):
@@ -110,7 +117,7 @@ def tile_koslmcell_pa_t_kernel(
 
         def warm(n):
             if n:
-                warm_out = psum.tile([P, H], F32, tag="acc_z")
+                warm_out = psum.tile([P, H], F32, **bank("acc_z", ACCZ))
                 for v in range(n):
                     nc.tensor.matmul(out=warm_out[:], lhsT=warm_in[:, 0:P], rhs=warm_in[:], start=True, stop=True)
 
@@ -176,10 +183,10 @@ def tile_koslmcell_pa_t_kernel(
 
         bias_z = const.tile([P, H], F32)
         bias_m = const.tile([P, BLOCKS], F32)
-        decay = psum.tile([P, H], F32, bufs=1)
+        decay = psum.tile([P, H], F32, bufs=1, name="decay") if DPS else psum.tile([P, H], F32, **bank("back", 2), name="decay")
 
         def set_up():
-            turned_rows = psum.tile([P, P], BF16, tag="back")
+            turned_rows = psum.tile([P, P], BF16, **bank("back", 2))
             nc.tensor.transpose(turned_rows[:], rows[:], ident_bf[:])
             cols = const.tile([P, 28], F32)
             nc.vector.tensor_copy(out=cols[:], in_=turned_rows[:, 0:28])
@@ -193,20 +200,20 @@ def tile_koslmcell_pa_t_kernel(
             live["lam"] = lam
 
         def set_up_2():
-            z_spread = psum.tile([P, H], F32, tag="acc_z")
+            z_spread = psum.tile([P, H], F32, **bank("acc_z", ACCZ))
             for j in range(BLOCKS):
                 nc.tensor.transpose(z_spread[:, j * P : (j + 1) * P], live["sums"][:, j : j + 1].to_broadcast([P, P]), ident[:])
             nc.vector.tensor_copy(out=bias_z[:], in_=z_spread[:])
             for j in range(BLOCKS):
                 nc.tensor.transpose(decay[:, j * P : (j + 1) * P], live["lam"][:, j : j + 1].to_broadcast([P, P]), ident[:])
-            if GD:
+            if GD or not DPS:
                 decay_sb = const.tile([P, H], F32)
-                nc.vector.tensor_copy(out=decay_sb[:], in_=decay[:])
+                (nc.scalar.copy if DSB else nc.vector.tensor_copy)(out=decay_sb[:], in_=decay[:])
                 live["decay_sb"] = decay_sb
 
         def transpose_tile(i):
             c, r = divmod(i, CHUNK)
-            turned = psum.tile([P, 2, 2, P], F32)
+            turned = psum.tile([P, 2, 2, P], F32, **bank("turned", 2))
             for a, name in enumerate(("x", "h")):
                 as_words = live[name, c][:, r, :].bitcast(F32)
                 for u in range(2):
@@ -259,7 +266,7 @@ def tile_koslmcell_pa_t_kernel(
         def multiply_z(i):
             c, r = divmod(i, CHUNK)
             batch = slice(r * P, (r + 1) * P)
-            acc_z = psum.tile([P, H], F32)
+            acc_z = psum.tile([P, H], F32, **bank("acc_z", ACCZ))
             for a, name in enumerate(("x", "h")):
                 nc.tensor.matmul_mx(
                     out=acc_z[:],
@@ -300,7 +307,7 @@ def tile_koslmcell_pa_t_kernel(
 
         def multiply_m(b):
             c, r0, nr, j0, nj = unit(b)
-            acc_t = psum.tile([P, nj, nr * P], F32, bufs=ACCT)
+            acc_t = psum.tile([P, nj, nr * P], F32, **bank("acc_t", ACCT))
             step = nr * P if nr == 4 else P
             for v in range(nj):
                 j = j0 + v
@@ -328,7 +335,7 @@ def tile_koslmcell_pa_t_kernel(
 
         def turn_back(b):
             c, r0, nr, j0, nj = unit(b)
-            back = psum.tile([P, nr, nj, P], F32)
+            back = psum.tile([P, nr, nj, P], F32, **bank("back", 2))
             for r in range(nr):
                 for v in range(nj):
                     nc.tensor.transpose(back[:, r, v, :], live["tanh_t", b][:, v, r * P : (r + 1) * P], ident[:])
@@ -372,7 +379,7 @@ def tile_koslmcell_pa_t_kernel(
                 nc.vector.tensor_tensor(
                     out=live["damped", c][:, r : r + n, :],
                     in0=live["c", c][:, r : r + n, :],
-                    in1=decay[:].unsqueeze(1).to_broadcast([P, n, H]),
+                    in1=(decay if DPS else live["decay_sb"])[:].unsqueeze(1).to_broadcast([P, n, H]),
                     op=MULT,
                 )
 

@@ -45,7 +45,7 @@ VECTOR_SUMS = 2
 ZW = 4
 VREG = (3,)
 QLAG = 1
-QSPLIT = 2
+QSPLIT = 1
 GD = (2,)
 DC = 2
 TZ = 1
@@ -56,21 +56,23 @@ VREG0 = (1, 3)
 WARM = 0
 WARM2 = 0
 GPV = 0
-LOADS = "xt0 ht0 xr hr vec x1 h1 px wx wh ph x2 h2 c0".split()
+LOADS = "xt0 ht0 xr hr vec x1 h1 px wx wh ph c0 x2 h2".split()
 QH = 0
 STYLE = [4] * 8
 MSTORE = [4] * 8
-SETUP = 3
+SETUP = 2
 SETUP2 = 4
 DSB = 1
 ACCT = 1
 BANKS = 7
+PAT = None
+THB = 3
 ACCZ = 2
 DPS = 1
 MBUF = 2
 IBUF = 3
 DBUF = 2
-ORDER = "T sm P B su Mm Mz tm bz qx qh tz dm su2 rg tot st".split()
+ORDER = "T sm P B su Mm Mz tm bz tz dm su2 rg tot qx qh st".split()
 
 FLOPS = 2 * BATCH * (2 * K) * (2 * H)
 
@@ -327,7 +329,7 @@ def tile_koslmcell_pa_t_kernel(
 
         def tanh_m(b):
             c, r0, nr, j0, nj = unit(b)
-            tanh_t = work.tile([P, nj, nr * P], F32, bufs=3)
+            tanh_t = work.tile([P, nj, nr * P], F32, bufs=THB)
             for v in range(nj):
                 j = j0 + v
                 nc.scalar.activation(out=tanh_t[:, v, :], in_=live["acc_t", b][:, v, :], func=ACT.Tanh, bias=live["sums"][:, BLOCKS + j : BLOCKS + j + 1])
@@ -424,12 +426,25 @@ def tile_koslmcell_pa_t_kernel(
             "rg": lambda s: run(regroup_tile, s - RGL),
             "sm": lambda s: run(scale_m, s - M_OUT),
             "st": lambda s: run(store_total, s - TOT),
+            "nop": lambda s: None,
             "su": lambda s: set_up() if s == SETUP else None,
             "su2": lambda s: set_up_2() if s == SETUP2 else None,
         }
         warm(WARM)
-        for s in range(STEPS):
-            if 0 < s < 5:
-                warm(WARM2)
-            for name in ORDER:
-                stages[name](s)
+        if PAT:
+            n = len(PAT)
+            for s in range(0, STEPS + n, n):
+                if s == 0:
+                    warm(WARM)
+                for d in range(n):
+                    for name in PAT[d]:
+                        dd = d
+                        if name not in stages:
+                            name, dd = name[:-1], int(name[-1])
+                        stages[name](s + dd)
+        else:
+            for s in range(STEPS):
+                if 0 < s < 5:
+                    warm(WARM2)
+                for name in ORDER:
+                    stages[name](s)

@@ -20,74 +20,65 @@ K = 512
 H = 512
 M_SCALE = 1.5
 TILES = BATCH // P
+PAIR = 2
 CHUNK = 4
 ROWS = CHUNK * P
 CHUNKS = TILES // CHUNK
 BLOCKS = H // P
 assert BLOCKS == CHUNK
 
-
-PAIR = 2
-HALF = PAIR * P
-QUANTISE = 2
+QUANTISE = 1
 Z_MULTIPLY = 5
 Z_BIAS = 6
 Z_TANH = 7
+DAMP = 6
 M_MULTIPLY = 8
 M_TANH = 9
 TURN_BACK = 10
 M_OUT = 11
 PRODUCT = 11
-DAMP = 6
-TOT = 12
-STEPS = TILES + 13
+TOTAL = 12
+STEPS = TILES + TOTAL
+SET_UP = 2
+SPREAD = 4
+
+PSUM_BANKS = 7
+VECTOR_COPIES_FIRST = (1, 3)
+VECTOR_COPIES = (3,)
+GPSIMD_DAMPS = 2
 VECTOR_SUMS = 2
-ZW = 4
-VREG = (3,)
-QLAG = 1
-QSPLIT = 1
-GD = (2,)
-DC = 2
-TZ = 1
-XB = 6
-QPAIRS = (0,)
-RGL = 0
-VREG0 = (1, 3)
-WARM = 0
-WARM2 = 0
-GPV = 0
-LOADS = "xt0 ht0 xr hr vec x1 h1 px wx wh ph c0 x2 h2".split()
-QH = 0
-STYLE = [4] * 8
-MSTORE = [4] * 8
-SETUP = 2
-SETUP2 = 4
-DSB = 1
-ACCT = 1
-BANKS = 7
-PAT = None
-THB = 3
-ACCZ = 2
-DPS = 1
-MBUF = 2
-IBUF = 3
-DBUF = 2
-ORDER = "T sm P B su Mm Mz tm bz tz dm su2 rg tot qx qh st".split()
+FINE_STORES = 3
+
+ROW_B_IH, ROW_B_HH, ROW_Z_BIAS, ROW_M_BIAS, ROW_LAMBDA, ROW_END = 0, 8, 16, 20, 24, 28
 
 FLOPS = 2 * BATCH * (2 * K) * (2 * H)
 
 
 def tile_koslmcell_pa_t_kernel(
-    tc, x, h_prev, c_prev, W_ih_words, W_ih_scales, b_ih, W_hh_words, W_hh_scales, b_hh,
-    log_lambda, z_bias, m_bias, out_0, out_1, out_2,
+    tc,
+    x,
+    h_prev,
+    c_prev,
+    W_ih_words,
+    W_ih_scales,
+    b_ih,
+    W_hh_words,
+    W_hh_scales,
+    b_hh,
+    log_lambda,
+    z_bias,
+    m_bias,
+    out_0,
+    out_1,
+    out_2,
 ):
     nc = tc.nc
-    x_v = x.rearrange("(p t) k -> p t k", t=TILES)
-    h_v = h_prev.rearrange("(p t) k -> p t k", t=TILES)
-    c_v = c_prev.rearrange("(p t) k -> p t k", t=TILES)
-    z_v = out_0.rearrange("(p t) k -> p t k", t=TILES)
-    m_v = out_1.rearrange("(p t) k -> p t k", t=TILES)
-    i_v = out_2.rearrange("(p t) k -> p t k", t=TILES)
+
+    def by_tile(array):
+        return array.rearrange("(p t) k -> p t k", t=TILES)
+
+    sources = {"x": by_tile(x), "h": by_tile(h_prev), "c": by_tile(c_prev)}
+    z_v, m_v, i_v = by_tile(out_0), by_tile(out_1), by_tile(out_2)
 
     def as_blocks(vector):
         return vector.rearrange("(j p) -> j p", p=P)
@@ -95,42 +86,24 @@ def tile_koslmcell_pa_t_kernel(
     with ExitStack() as ctx:
         ctx.enter_context(tc.manual_schedule())
         const = ctx.enter_context(tc.tile_pool(name="const", bufs=1))
-        inputs = ctx.enter_context(tc.tile_pool(name="inputs", bufs=1))
+        inputs = ctx.enter_context(tc.tile_pool(name="inputs", bufs=3))
         work = ctx.enter_context(tc.tile_pool(name="work", bufs=2))
         stores = ctx.enter_context(tc.tile_pool(name="stores", bufs=2))
-        psum = ctx.enter_context(tc.psum_pool(name="psum", bufs=2))
+        psum = ctx.enter_context(tc.psum_pool(name="psum", bufs=PSUM_BANKS))
 
         live = {}
 
-        def bank(tag, bufs):
-            return {"tag": "bank", "bufs": BANKS} if BANKS else {"tag": tag, "bufs": bufs}
-        views = {"x": x_v, "h": h_v, "c": c_v}
-
-        def load(name, c, lo=0, hi=CHUNK):
-            if (name, c) not in live:
-                held = inputs.tile([P, CHUNK, K], BF16, name="in_" + name, bufs=XB)
-                live[name, c] = held
-            nc.sync.dma_start(out=live[name, c][:, lo:hi, :], in_=views[name][:, c * CHUNK + lo : c * CHUNK + hi, :])
-
         ident = const.tile([P, P], F32)
         make_identity(nc, ident[:])
-        warm_in = const.tile([P, 512], BF16)
-        nc.vector.memset(warm_in[:].bitcast(I32), 0)
-
-        def warm(n):
-            if n:
-                warm_out = psum.tile([P, H], F32, **bank("acc_z", ACCZ))
-                for v in range(n):
-                    nc.tensor.matmul(out=warm_out[:], lhsT=warm_in[:, 0:P], rhs=warm_in[:], start=True, stop=True)
-
         ident_bf = const.tile([P, P], BF16)
-        words = {}
-        planes = {}
-        srcs = {"x": (W_ih_words, W_ih_scales), "h": (W_hh_words, W_hh_scales)}
+        make_identity(nc, ident_bf[:])
         spark = const.tile([P, 1], F32)
         nc.vector.memset(spark[:], 0.0)
         sparked = const.tile([P, 1], F32)
         nc.scalar.activation(out=sparked[:], in_=spark[:], func=ACT.Tanh)
+        words = {}
+        planes = {}
+        weights = {"x": (W_ih_words, W_ih_scales), "h": (W_hh_words, W_hh_scales)}
         for name in ("x", "h"):
             w_sb = const.tile([P, 4 * H], U8, name="words_" + name, align_bytes=64)
             words[name] = w_sb
@@ -140,84 +113,92 @@ def tile_koslmcell_pa_t_kernel(
         rows = const.tile([P, P], BF16)
         nc.vector.memset(rows[:].bitcast(I32), 0)
 
+        def part(name, i):
+            return live[name, i // (2 * CHUNK)], i % (2 * CHUNK)
+
+        def load(name, lo, hi):
+            if lo % (2 * CHUNK) == 0:
+                held = inputs.tile([P, 2 * CHUNK, K], BF16, name="in_" + name)
+                live[name, lo // (2 * CHUNK)] = held
+            tile, at = part(name, lo)
+            nc.sync.dma_start(out=tile[:, at : at + hi - lo, :], in_=sources[name][:, lo:hi, :])
+
         def load_words(name):
-            nc.sync.dma_start(out=words[name][:].bitcast(I32), in_=srcs[name][0][0].bitcast(I32))
+            nc.sync.dma_start(out=words[name][:].bitcast(I32), in_=weights[name][0][0].bitcast(I32))
 
         def load_plane(name):
             for quad in range(4):
                 nc.sync.dma_start(
                     out=planes[name][32 * quad : 32 * quad + 4, :].bitcast(I32),
-                    in_=srcs[name][1][0, 4 * quad : 4 * quad + 4, :].bitcast(I32),
+                    in_=weights[name][1][0, 4 * quad : 4 * quad + 4, :].bitcast(I32),
                 )
 
         def load_vectors():
-            q = nc.gpsimd if GPV else nc.sync
-            q.dma_start(out=rows[0:8, :], in_=as_blocks(b_ih))
-            q.dma_start(out=rows[8:16, :], in_=as_blocks(b_hh))
-            q.dma_start(out=rows[16:20, :], in_=as_blocks(z_bias))
-            q.dma_start(out=rows[20:24, :], in_=as_blocks(m_bias))
-            q.dma_start(out=rows[24:28, :], in_=as_blocks(log_lambda))
+            for vector, lo, hi in (
+                (b_ih, ROW_B_IH, ROW_B_HH),
+                (b_hh, ROW_B_HH, ROW_Z_BIAS),
+                (z_bias, ROW_Z_BIAS, ROW_M_BIAS),
+                (m_bias, ROW_M_BIAS, ROW_LAMBDA),
+                (log_lambda, ROW_LAMBDA, ROW_END),
+            ):
+                nc.sync.dma_start(out=rows[lo:hi, :], in_=as_blocks(vector))
 
-        if GPV:
-            load_vectors()
-        make_identity(nc, ident_bf[:])
-        table = {
-            "xt0": lambda: load("x", 0, 0, 1), "ht0": lambda: load("h", 0, 0, 1),
-            "xr": lambda: load("x", 0, 1, 4), "hr": lambda: load("h", 0, 1, 4),
-            "x0": lambda: load("x", 0), "h0": lambda: load("h", 0),
-            "xa": lambda: load("x", 0, 0, 2), "ha": lambda: load("h", 0, 0, 2),
-            "xb": lambda: load("x", 0, 2, 4), "hb": lambda: load("h", 0, 2, 4),
-            "px": lambda: load_plane("x"), "ph": lambda: load_plane("h"),
-            "wx": lambda: load_words("x"), "wh": lambda: load_words("h"),
-            "vec": lambda: None if GPV else load_vectors(),
-        }
-        for name in LOADS:
-            if name in table:
-                table[name]()
-            else:
-                load(name[0], int(name[1]))
-        for c in range(2, CHUNKS):
+        for lo, hi in ((0, 1), (1, CHUNK)):
+            load("x", lo, hi)
+            load("h", lo, hi)
+        load_vectors()
+        load("x", CHUNK, 2 * CHUNK)
+        load("h", CHUNK, 2 * CHUNK)
+        load_plane("x")
+        load_words("x")
+        load_words("h")
+        load_plane("h")
+        load("c", 0, CHUNK)
+        for lo in (2 * CHUNK, 3 * CHUNK):
+            load("x", lo, lo + CHUNK)
+            load("h", lo, lo + CHUNK)
+            load("c", lo - CHUNK, lo)
+        load("c", 3 * CHUNK, 4 * CHUNK)
+        for lo in range(4 * CHUNK, TILES, 2 * CHUNK):
             for name in ("x", "h", "c"):
-                k = c if name != "c" else c - 1
-                if (name, k) not in live:
-                    load(name, k)
-        load("c", CHUNKS - 1)
+                load(name, lo, lo + 2 * CHUNK)
 
         bias_z = const.tile([P, H], F32)
-        bias_m = const.tile([P, BLOCKS], F32)
-        decay = psum.tile([P, H], F32, bufs=1, name="decay") if DPS else psum.tile([P, H], F32, **bank("back", 2), name="decay")
+        decay = psum.tile([P, H], F32, bufs=1)
+        decay_sb = const.tile([P, H], F32)
+        sums = const.tile([P, 2 * BLOCKS], F32)
+        exp_lambda = const.tile([P, BLOCKS], F32)
+
+        def bank(shape, dtype, name):
+            return psum.tile(shape, dtype, name=name, tag="bank")
 
         def set_up():
-            turned_rows = psum.tile([P, P], BF16, **bank("back", 2))
+            turned_rows = bank([P, P], BF16, "turned_rows")
             nc.tensor.transpose(turned_rows[:], rows[:], ident_bf[:])
-            cols = const.tile([P, 28], F32)
-            nc.vector.tensor_copy(out=cols[:], in_=turned_rows[:, 0:28])
-            both = const.tile([P, 8], F32)
-            nc.vector.tensor_tensor(out=both[:], in0=cols[:, 0:8], in1=cols[:, 8:16], op=ADD)
-            sums = const.tile([P, 8], F32)
-            nc.vector.tensor_tensor(out=sums[:], in0=both[:], in1=cols[:, 16:24], op=ADD)
-            lam = const.tile([P, BLOCKS], F32)
-            nc.scalar.activation(out=lam[:], in_=cols[:, 24:28], func=ACT.Exp)
-            live["sums"] = sums
-            live["lam"] = lam
+            cols = const.tile([P, ROW_END], F32)
+            nc.vector.tensor_copy(out=cols[:], in_=turned_rows[:, 0:ROW_END])
+            both = const.tile([P, 2 * BLOCKS], F32)
+            nc.vector.tensor_tensor(out=both[:], in0=cols[:, ROW_B_IH:ROW_B_HH], in1=cols[:, ROW_B_HH:ROW_Z_BIAS], op=ADD)
+            nc.vector.tensor_tensor(out=sums[:], in0=both[:], in1=cols[:, ROW_Z_BIAS:ROW_LAMBDA], op=ADD)
+            nc.scalar.activation(out=exp_lambda[:], in_=cols[:, ROW_LAMBDA:ROW_END], func=ACT.Exp)
 
-        def set_up_2():
-            z_spread = psum.tile([P, H], F32, **bank("acc_z", ACCZ))
+        def spread(out, column):
+            nc.tensor.transpose(out, column.to_broadcast([P, P]), ident[:])
+
+        def spread_vectors():
+            z_spread = bank([P, H], F32, "z_spread")
             for j in range(BLOCKS):
-                nc.tensor.transpose(z_spread[:, j * P : (j + 1) * P], live["sums"][:, j : j + 1].to_broadcast([P, P]), ident[:])
+                spread(z_spread[:, j * P : (j + 1) * P], sums[:, j : j + 1])
             nc.vector.tensor_copy(out=bias_z[:], in_=z_spread[:])
             for j in range(BLOCKS):
-                nc.tensor.transpose(decay[:, j * P : (j + 1) * P], live["lam"][:, j : j + 1].to_broadcast([P, P]), ident[:])
-            if GD or not DPS:
-                decay_sb = const.tile([P, H], F32)
-                (nc.scalar.copy if DSB else nc.vector.tensor_copy)(out=decay_sb[:], in_=decay[:])
-                live["decay_sb"] = decay_sb
+                spread(decay[:, j * P : (j + 1) * P], exp_lambda[:, j : j + 1])
+            nc.scalar.copy(out=decay_sb[:], in_=decay[:])
 
         def transpose_tile(i):
-            c, r = divmod(i, CHUNK)
-            turned = psum.tile([P, 2, 2, P], F32, **bank("turned", 2))
+            turned = bank([P, 2, 2, P], F32, "turned")
             for a, name in enumerate(("x", "h")):
-                as_words = live[name, c][:, r, :].bitcast(F32)
+                tile, at = part(name, i)
+                as_words = tile[:, at, :].bitcast(F32)
                 for u in range(2):
                     nc.tensor.transpose(turned[:, a, u, :], as_words[:, u : K // 2 : 2], ident[:])
             live["turned", i] = turned
@@ -225,50 +206,41 @@ def tile_koslmcell_pa_t_kernel(
         def regroup_tile(i):
             c, r = divmod(i, CHUNK)
             if r == 0:
-                grouped = work.tile([P, 2, ROWS, 4], BF16, bufs=2, align_bytes=64)
+                grouped = work.tile([P, 2, ROWS, 4], BF16, align_bytes=64)
                 live["grouped", c] = grouped
-            copier = nc.vector.tensor_copy if r in (VREG0 if c == 0 else VREG) else nc.scalar.copy
+            by_vector = VECTOR_COPIES_FIRST if c == 0 else VECTOR_COPIES
+            copier = nc.vector.tensor_copy if r in by_vector else nc.scalar.copy
             copier(
                 out=live["grouped", c][:, :, r * P : (r + 1) * P, :].bitcast(F32),
                 in_=live["turned", i][:].rearrange("p a u r -> p a r u"),
             )
 
-        def quantise(c, a0, a1, lo, hi):
-            if ("codes", c) not in live:
+        def quantise(i):
+            c, r = divmod(i, CHUNK)
+            if r == (1 if c == 0 else CHUNK - 1):
                 codes = work.tile([P, 2, ROWS], U32, bufs=3, align_bytes=64)
                 scales = work.tile([P, 2, ROWS], U8, bufs=3, align_bytes=64)
                 live["codes", c] = codes
                 live["scales", c] = scales
-            if a1 - a0 == 2:
+            if c == 0 and r % PAIR == PAIR - 1:
+                batch = slice((r + 1 - PAIR) * P, (r + 1) * P)
+                for a in range(2):
+                    nc.vector.quantize_mx(
+                        out=live["codes", c][:, a, batch].bitcast(FP8X4),
+                        scales=live["scales", c][:, a, batch],
+                        in_=live["grouped", c][:, a, batch, :].rearrange("p r t -> p (r t)"),
+                    )
+            elif c > 0 and r == CHUNK - 1:
                 nc.vector.quantize_mx(
                     out=live["codes", c][:].rearrange("p a r -> p (a r)").bitcast(FP8X4),
                     scales=live["scales", c][:].rearrange("p a r -> p (a r)"),
                     in_=live["grouped", c][:].rearrange("p a r t -> p (a r t)"),
                 )
-            else:
-                nc.vector.quantize_mx(
-                    out=live["codes", c][:, a0, lo:hi].bitcast(FP8X4),
-                    scales=live["scales", c][:, a0, lo:hi],
-                    in_=live["grouped", c][:, a0, lo:hi, :].rearrange("p r t -> p (r t)"),
-                )
-
-        def quantise_step(s, part):
-            c, r = divmod(s, CHUNK)
-            if not 0 <= c < CHUNKS:
-                return
-            if c in QPAIRS:
-                if r % 2 == 1:
-                    quantise(c, part, part + 1, (r - 1) * P, (r + 1) * P)
-            elif r == 3:
-                if QSPLIT == 2:
-                    quantise(c, part, part + 1, 0, ROWS)
-                elif part == 0:
-                    quantise(c, 0, 2, 0, ROWS)
 
         def multiply_z(i):
             c, r = divmod(i, CHUNK)
             batch = slice(r * P, (r + 1) * P)
-            acc_z = psum.tile([P, H], F32, **bank("acc_z", ACCZ))
+            acc_z = bank([P, H], F32, "acc_z")
             for a, name in enumerate(("x", "h")):
                 nc.tensor.matmul_mx(
                     out=acc_z[:],
@@ -282,169 +254,127 @@ def tile_koslmcell_pa_t_kernel(
             live["acc_z", i] = acc_z
 
         def add_bias_z(i):
-            g = i % TZ
-            if g == 0:
-                pre_z = work.tile([P, TZ, H], F32, bufs=3)
-                live["pre_z", i] = pre_z
-            nc.vector.tensor_tensor(out=live["pre_z", i - g][:, g, :], in0=live["acc_z", i][:], in1=bias_z[:], op=ADD)
+            pre_z = work.tile([P, H], F32, bufs=3)
+            nc.vector.tensor_tensor(out=pre_z[:], in0=live["acc_z", i][:], in1=bias_z[:], op=ADD)
+            live["pre_z", i] = pre_z
 
         def tanh_z(i):
             c, r = divmod(i, CHUNK)
             if r == 0:
                 z_st = stores.tile([P, CHUNK, H], F32, bufs=3)
                 live["z", c] = z_st
-            if i % TZ == 0:
-                nc.scalar.activation(out=live["z", c][:, r : r + TZ, :], in_=live["pre_z", i][:], func=ACT.Tanh)
-                w = min(ZW, 2) if c == CHUNKS - 1 else ZW
-                e = r + TZ
-                if e % w == 0:
-                    nc.sync.dma_start(out=z_v[:, c * CHUNK + e - w : c * CHUNK + e, :], in_=live["z", c][:, e - w : e, :])
-
-        def unit(b):
-            c, k = divmod(b, CHUNK)
-            n = STYLE[c]
-            if n == 4:
-                return c, 0, 4, k, 1
-            return c, 2 * (k // 2), 2, 2 * (k % 2), 2
+            nc.scalar.activation(out=live["z", c][:, r, :], in_=live["pre_z", i][:], func=ACT.Tanh)
+            n = PAIR if c >= CHUNKS - FINE_STORES else CHUNK
+            if (r + 1) % n == 0:
+                nc.sync.dma_start(out=z_v[:, i + 1 - n : i + 1, :], in_=live["z", c][:, r + 1 - n : r + 1, :])
 
         def multiply_m(b):
-            c, r0, nr, j0, nj = unit(b)
-            acc_t = psum.tile([P, nj, nr * P], F32, **bank("acc_t", ACCT))
-            step = nr * P if nr == 4 else P
-            for v in range(nj):
-                j = j0 + v
-                for lo in range(0, nr * P, step):
-                    for a, name in enumerate(("x", "h")):
-                        cols = slice(r0 * P + lo, r0 * P + lo + step)
-                        nc.tensor.matmul_mx(
-                            out=acc_t[:, v, lo : lo + step],
-                            lhsT=words[name][:, 2 * (H + j * P) : 2 * (H + (j + 1) * P)].bitcast(FP4X4),
-                            lhsT_scale=planes[name][:, H + j * P : H + (j + 1) * P],
-                            rhs=live["codes", c][:, a, cols].bitcast(FP8X4),
-                            rhs_scale=live["scales", c][:, a, cols],
-                            start=(a == 0),
-                            stop=(a == 1),
-                        )
+            c, j = divmod(b, BLOCKS)
+            acc_t = bank([P, ROWS], F32, "acc_t")
+            for a, name in enumerate(("x", "h")):
+                nc.tensor.matmul_mx(
+                    out=acc_t[:],
+                    lhsT=words[name][:, 2 * (H + j * P) : 2 * (H + (j + 1) * P)].bitcast(FP4X4),
+                    lhsT_scale=planes[name][:, H + j * P : H + (j + 1) * P],
+                    rhs=live["codes", c][:, a, :].bitcast(FP8X4),
+                    rhs_scale=live["scales", c][:, a, :],
+                    start=(a == 0),
+                    stop=(a == 1),
+                )
             live["acc_t", b] = acc_t
 
         def tanh_m(b):
-            c, r0, nr, j0, nj = unit(b)
-            tanh_t = work.tile([P, nj, nr * P], F32, bufs=THB)
-            for v in range(nj):
-                j = j0 + v
-                nc.scalar.activation(out=tanh_t[:, v, :], in_=live["acc_t", b][:, v, :], func=ACT.Tanh, bias=live["sums"][:, BLOCKS + j : BLOCKS + j + 1])
+            j = b % BLOCKS
+            tanh_t = work.tile([P, ROWS], F32, bufs=3)
+            nc.scalar.activation(
+                out=tanh_t[:], in_=live["acc_t", b][:], func=ACT.Tanh, bias=sums[:, BLOCKS + j : BLOCKS + j + 1]
+            )
             live["tanh_t", b] = tanh_t
 
         def turn_back(b):
-            c, r0, nr, j0, nj = unit(b)
-            back = psum.tile([P, nr, nj, P], F32, **bank("back", 2))
-            for r in range(nr):
-                for v in range(nj):
-                    nc.tensor.transpose(back[:, r, v, :], live["tanh_t", b][:, v, r * P : (r + 1) * P], ident[:])
+            back = bank([P, CHUNK, P], F32, "back")
+            for r in range(CHUNK):
+                nc.tensor.transpose(back[:, r, :], live["tanh_t", b][:, r * P : (r + 1) * P], ident[:])
             live["back", b] = back
 
-        def area(b):
-            c, r0, nr, j0, nj = unit(b)
-            return slice(r0, r0 + nr), slice(j0 * P, (j0 + nj) * P)
-
-        def store_unit(view, held, b):
-            c, r0, nr, j0, nj = unit(b)
-            if nr == 2:
-                if j0 == 2:
-                    nc.sync.dma_start(out=view[:, c * CHUNK + r0 : c * CHUNK + r0 + 2, :], in_=held[:, r0 : r0 + 2, :])
-            else:
-                w = MSTORE[c]
-                if (j0 + 1) % w == 0:
-                    cols = slice((j0 + 1 - w) * P, (j0 + 1) * P)
-                    nc.sync.dma_start(out=view[:, c * CHUNK : (c + 1) * CHUNK, cols], in_=held[:, :, cols])
+        def store_blocks(view, held, c, j):
+            n = BLOCKS // 2 if c >= CHUNKS - FINE_STORES else BLOCKS
+            if (j + 1) % n == 0:
+                cols = slice((j + 1 - n) * P, (j + 1) * P)
+                nc.sync.dma_start(out=view[:, c * CHUNK : (c + 1) * CHUNK, cols], in_=held[:, :, cols])
 
         def scale_m(b):
-            c, k = divmod(b, CHUNK)
-            if k == 0:
-                m_st = stores.tile([P, CHUNK, H], F32, bufs=MBUF)
+            c, j = divmod(b, BLOCKS)
+            if j == 0:
+                m_st = stores.tile([P, CHUNK, H], F32)
                 live["m", c] = m_st
-            rs, cs = area(b)
-            nc.scalar.mul(live["m", c][:, rs, cs], live["back", b][:].rearrange("p r v n -> p r (v n)"), M_SCALE)
-            store_unit(m_v, live["m", c], b)
+            nc.scalar.mul(live["m", c][:, :, j * P : (j + 1) * P], live["back", b][:], M_SCALE)
+            store_blocks(m_v, live["m", c], c, j)
 
         def damp_cell(i):
             c, r = divmod(i, CHUNK)
             if r == 0:
-                damped = work.tile([P, CHUNK, H], F32, bufs=DBUF)
+                damped = work.tile([P, CHUNK, H], F32)
                 live["damped", c] = damped
-            if r in GD:
-                nc.gpsimd.tensor_tensor(out=live["damped", c][:, r, :], in0=live["c", c][:, r, :], in1=live["decay_sb"][:], op=MULT)
-            elif (r % DC == 0) or ((r - 1) in GD):
-                n = DC
-                while any((r + v) in GD or r + v >= CHUNK for v in range(n)):
-                    n -= 1
+            tile, at = part("c", i)
+            if r == GPSIMD_DAMPS:
+                nc.gpsimd.tensor_tensor(out=live["damped", c][:, r, :], in0=tile[:, at, :], in1=decay_sb[:], op=MULT)
+            elif r == 0 or r > GPSIMD_DAMPS:
+                n = GPSIMD_DAMPS if r == 0 else 1
                 nc.vector.tensor_tensor(
                     out=live["damped", c][:, r : r + n, :],
-                    in0=live["c", c][:, r : r + n, :],
-                    in1=(decay if DPS else live["decay_sb"])[:].unsqueeze(1).to_broadcast([P, n, H]),
+                    in0=tile[:, at : at + n, :],
+                    in1=decay[:].unsqueeze(1).to_broadcast([P, n, H]),
                     op=MULT,
                 )
 
         def product(b):
-            c, k = divmod(b, CHUNK)
-            if k == 0:
-                i_st = stores.tile([P, CHUNK, H], F32, bufs=IBUF)
+            c, j = divmod(b, BLOCKS)
+            if j == 0:
+                i_st = stores.tile([P, CHUNK, H], F32, bufs=3)
                 live["i", c] = i_st
-            rs, cs = area(b)
-            nc.vector.scalar_tensor_tensor(out=live["i", c][:, rs, cs], in0=live["back", b][:].rearrange("p r v n -> p r (v n)"), scalar=M_SCALE, in1=live["damped", c][:, rs, cs], op0=MULT, op1=MULT)
+            cols = slice(j * P, (j + 1) * P)
+            nc.vector.scalar_tensor_tensor(
+                out=live["i", c][:, :, cols],
+                in0=live["back", b][:],
+                scalar=M_SCALE,
+                in1=live["damped", c][:, :, cols],
+                op0=MULT,
+                op1=MULT,
+            )
 
         def total(b):
-            c, k = divmod(b, CHUNK)
-            rs, cs = area(b)
+            c, j = divmod(b, BLOCKS)
+            cols = slice(j * P, (j + 1) * P)
             adder = nc.vector if b >= TILES - VECTOR_SUMS else nc.gpsimd
-            adder.tensor_tensor(out=live["i", c][:, rs, cs], in0=live["i", c][:, rs, cs], in1=live["z", c][:, rs, cs], op=ADD)
+            adder.tensor_tensor(
+                out=live["i", c][:, :, cols], in0=live["i", c][:, :, cols], in1=live["z", c][:, :, cols], op=ADD
+            )
 
         def store_total(b):
-            store_unit(i_v, live["i", b // CHUNK], b)
+            c, j = divmod(b, BLOCKS)
+            store_blocks(i_v, live["i", c], c, j)
 
         def run(stage, i):
             if 0 <= i < TILES:
                 stage(i)
 
-        def run_pair(stage, i):
-            if i % PAIR == 0:
-                run(stage, i)
-
-        stages = {
-            "T": lambda s: run(transpose_tile, s),
-            "B": lambda s: run(turn_back, s - TURN_BACK),
-            "Mm": lambda s: run(multiply_m, s - M_MULTIPLY),
-            "Mz": lambda s: run(multiply_z, s - Z_MULTIPLY),
-            "P": lambda s: run(product, s - PRODUCT),
-            "tot": lambda s: run(total, s - TOT),
-            "qx": lambda s: quantise_step(s - QLAG, 0),
-            "qh": lambda s: quantise_step(s - QLAG, 1),
-            "bz": lambda s: run(add_bias_z, s - Z_BIAS),
-            "dm": lambda s: run(damp_cell, s - DAMP),
-            "tm": lambda s: run(tanh_m, s - M_TANH),
-            "tz": lambda s: run(tanh_z, s - Z_TANH),
-            "rg": lambda s: run(regroup_tile, s - RGL),
-            "sm": lambda s: run(scale_m, s - M_OUT),
-            "st": lambda s: run(store_total, s - TOT),
-            "nop": lambda s: None,
-            "su": lambda s: set_up() if s == SETUP else None,
-            "su2": lambda s: set_up_2() if s == SETUP2 else None,
-        }
-        warm(WARM)
-        if PAT:
-            n = len(PAT)
-            for s in range(0, STEPS + n, n):
-                if s == 0:
-                    warm(WARM)
-                for d in range(n):
-                    for name in PAT[d]:
-                        dd = d
-                        if name not in stages:
-                            name, dd = name[:-1], int(name[-1])
-                        stages[name](s + dd)
-        else:
-            for s in range(STEPS):
-                if 0 < s < 5:
-                    warm(WARM2)
-                for name in ORDER:
-                    stages[name](s)
+        for s in range(STEPS):
+            run(transpose_tile, s)
+            run(scale_m, s - M_OUT)
+            run(product, s - PRODUCT)
+            run(turn_back, s - TURN_BACK)
+            if s == SET_UP:
+                set_up()
+            run(multiply_m, s - M_MULTIPLY)
+            run(multiply_z, s - Z_MULTIPLY)
+            run(tanh_m, s - M_TANH)
+            run(add_bias_z, s - Z_BIAS)
+            run(tanh_z, s - Z_TANH)
+            run(damp_cell, s - DAMP)
+            if s == SPREAD:
+                spread_vectors()
+            run(regroup_tile, s)
+            run(total, s - TOTAL)
+            run(quantise, s - QUANTISE)
+            run(store_total, s - TOTAL)

from contextlib import ExitStack

import concourse.mybir as mybir
from concourse.masks import make_identity

F32 = mybir.dt.float32
BF16 = mybir.dt.bfloat16
I32 = mybir.dt.int32
U32 = mybir.dt.uint32
U8 = mybir.dt.uint8
FP8X4 = mybir.dt.float8_e4m3fn_x4
FP4X4 = mybir.dt.float4_e2m1fn_x4
ADD = mybir.AluOpType.add
MULT = mybir.AluOpType.mult
ACT = mybir.ActivationFunctionType

P = 128
BATCH = 4096
K = 512
H = 512
M_SCALE = 1.5
TILES = BATCH // P
PAIR = 2
CHUNK = 4
ROWS = CHUNK * P
CHUNKS = TILES // CHUNK
BLOCKS = H // P
assert BLOCKS == CHUNK

QUANTISE = 1
Z_MULTIPLY = 5
Z_BIAS = 6
Z_TANH = 7
DAMP = 6
M_MULTIPLY = 8
M_TANH = 9
TURN_BACK = 10
M_OUT = 11
PRODUCT = 11
TOTAL = 12
STEPS = TILES + TOTAL
SET_UP = 2
SPREAD = 4

PSUM_BANKS = 7
VECTOR_COPIES_FIRST = (1, 3)
VECTOR_COPIES = (3,)
GPSIMD_DAMPS = 2
VECTOR_SUMS = 2
FINE_STORES = 3

ROW_B_IH, ROW_B_HH, ROW_Z_BIAS, ROW_M_BIAS, ROW_LAMBDA, ROW_END = 0, 8, 16, 20, 24, 28

FLOPS = 2 * BATCH * (2 * K) * (2 * H)


def tile_koslmcell_pa_t_kernel(
    tc,
    x,
    h_prev,
    c_prev,
    W_ih_words,
    W_ih_scales,
    b_ih,
    W_hh_words,
    W_hh_scales,
    b_hh,
    log_lambda,
    z_bias,
    m_bias,
    out_0,
    out_1,
    out_2,
):
    nc = tc.nc

    def by_tile(array):
        return array.rearrange("(p t) k -> p t k", t=TILES)

    sources = {"x": by_tile(x), "h": by_tile(h_prev), "c": by_tile(c_prev)}
    z_v, m_v, i_v = by_tile(out_0), by_tile(out_1), by_tile(out_2)

    def as_blocks(vector):
        return vector.rearrange("(j p) -> j p", p=P)

    with ExitStack() as ctx:
        ctx.enter_context(tc.manual_schedule())
        const = ctx.enter_context(tc.tile_pool(name="const", bufs=1))
        inputs = ctx.enter_context(tc.tile_pool(name="inputs", bufs=3))
        work = ctx.enter_context(tc.tile_pool(name="work", bufs=2))
        stores = ctx.enter_context(tc.tile_pool(name="stores", bufs=2))
        psum = ctx.enter_context(tc.psum_pool(name="psum", bufs=PSUM_BANKS))

        live = {}

        ident = const.tile([P, P], F32)
        make_identity(nc, ident[:])
        ident_bf = const.tile([P, P], BF16)
        make_identity(nc, ident_bf[:])
        spark = const.tile([P, 1], F32)
        nc.vector.memset(spark[:], 0.0)
        sparked = const.tile([P, 1], F32)
        nc.scalar.activation(out=sparked[:], in_=spark[:], func=ACT.Tanh)
        words = {}
        planes = {}
        weights = {"x": (W_ih_words, W_ih_scales), "h": (W_hh_words, W_hh_scales)}
        for name in ("x", "h"):
            w_sb = const.tile([P, 4 * H], U8, name="words_" + name, align_bytes=64)
            words[name] = w_sb
            plane = const.tile([P, 2 * H], U8, name="plane_" + name, align_bytes=64)
            nc.vector.memset(plane[:].bitcast(I32), 0)
            planes[name] = plane
        rows = const.tile([P, P], BF16)
        nc.vector.memset(rows[:].bitcast(I32), 0)

        def part(name, i):
            return live[name, i // (2 * CHUNK)], i % (2 * CHUNK)

        def load(name, lo, hi):
            if lo % (2 * CHUNK) == 0:
                held = inputs.tile([P, 2 * CHUNK, K], BF16, name="in_" + name)
                live[name, lo // (2 * CHUNK)] = held
            tile, at = part(name, lo)
            nc.sync.dma_start(out=tile[:, at : at + hi - lo, :], in_=sources[name][:, lo:hi, :])

        def load_words(name):
            nc.sync.dma_start(out=words[name][:].bitcast(I32), in_=weights[name][0][0].bitcast(I32))

        def load_plane(name):
            for quad in range(4):
                nc.sync.dma_start(
                    out=planes[name][32 * quad : 32 * quad + 4, :].bitcast(I32),
                    in_=weights[name][1][0, 4 * quad : 4 * quad + 4, :].bitcast(I32),
                )

        def load_vectors():
            for vector, lo, hi in (
                (b_ih, ROW_B_IH, ROW_B_HH),
                (b_hh, ROW_B_HH, ROW_Z_BIAS),
                (z_bias, ROW_Z_BIAS, ROW_M_BIAS),
                (m_bias, ROW_M_BIAS, ROW_LAMBDA),
                (log_lambda, ROW_LAMBDA, ROW_END),
            ):
                nc.sync.dma_start(out=rows[lo:hi, :], in_=as_blocks(vector))

        for lo, hi in ((0, 1), (1, CHUNK)):
            load("x", lo, hi)
            load("h", lo, hi)
        load_vectors()
        load("x", CHUNK, 2 * CHUNK)
        load("h", CHUNK, 2 * CHUNK)
        load_plane("x")
        load_words("x")
        load_words("h")
        load_plane("h")
        load("c", 0, CHUNK)
        for lo in (2 * CHUNK, 3 * CHUNK):
            load("x", lo, lo + CHUNK)
            load("h", lo, lo + CHUNK)
            load("c", lo - CHUNK, lo)
        load("c", 3 * CHUNK, 4 * CHUNK)
        for lo in range(4 * CHUNK, TILES, 2 * CHUNK):
            for name in ("x", "h", "c"):
                load(name, lo, lo + 2 * CHUNK)

        bias_z = const.tile([P, H], F32)
        decay = psum.tile([P, H], F32, bufs=1)
        decay_sb = const.tile([P, H], F32)
        sums = const.tile([P, 2 * BLOCKS], F32)
        exp_lambda = const.tile([P, BLOCKS], F32)

        def bank(shape, dtype, name):
            return psum.tile(shape, dtype, name=name, tag="bank")

        def set_up():
            turned_rows = bank([P, P], BF16, "turned_rows")
            nc.tensor.transpose(turned_rows[:], rows[:], ident_bf[:])
            cols = const.tile([P, ROW_END], F32)
            nc.vector.tensor_copy(out=cols[:], in_=turned_rows[:, 0:ROW_END])
            both = const.tile([P, 2 * BLOCKS], F32)
            nc.vector.tensor_tensor(out=both[:], in0=cols[:, ROW_B_IH:ROW_B_HH], in1=cols[:, ROW_B_HH:ROW_Z_BIAS], op=ADD)
            nc.vector.tensor_tensor(out=sums[:], in0=both[:], in1=cols[:, ROW_Z_BIAS:ROW_LAMBDA], op=ADD)
            nc.scalar.activation(out=exp_lambda[:], in_=cols[:, ROW_LAMBDA:ROW_END], func=ACT.Exp)

        def spread(out, column):
            nc.tensor.transpose(out, column.to_broadcast([P, P]), ident[:])

        def spread_vectors():
            z_spread = bank([P, H], F32, "z_spread")
            for j in range(BLOCKS):
                spread(z_spread[:, j * P : (j + 1) * P], sums[:, j : j + 1])
            nc.vector.tensor_copy(out=bias_z[:], in_=z_spread[:])
            for j in range(BLOCKS):
                spread(decay[:, j * P : (j + 1) * P], exp_lambda[:, j : j + 1])
            nc.scalar.copy(out=decay_sb[:], in_=decay[:])

        def transpose_tile(i):
            turned = bank([P, 2, 2, P], F32, "turned")
            for a, name in enumerate(("x", "h")):
                tile, at = part(name, i)
                as_words = tile[:, at, :].bitcast(F32)
                for u in range(2):
                    nc.tensor.transpose(turned[:, a, u, :], as_words[:, u : K // 2 : 2], ident[:])
            live["turned", i] = turned

        def regroup_tile(i):
            c, r = divmod(i, CHUNK)
            if r == 0:
                grouped = work.tile([P, 2, ROWS, 4], BF16, align_bytes=64)
                live["grouped", c] = grouped
            by_vector = VECTOR_COPIES_FIRST if c == 0 else VECTOR_COPIES
            copier = nc.vector.tensor_copy if r in by_vector else nc.scalar.copy
            copier(
                out=live["grouped", c][:, :, r * P : (r + 1) * P, :].bitcast(F32),
                in_=live["turned", i][:].rearrange("p a u r -> p a r u"),
            )

        def quantise(i):
            c, r = divmod(i, CHUNK)
            if r == (1 if c == 0 else CHUNK - 1):
                codes = work.tile([P, 2, ROWS], U32, bufs=3, align_bytes=64)
                scales = work.tile([P, 2, ROWS], U8, bufs=3, align_bytes=64)
                live["codes", c] = codes
                live["scales", c] = scales
            if c == 0 and r % PAIR == PAIR - 1:
                batch = slice((r + 1 - PAIR) * P, (r + 1) * P)
                for a in range(2):
                    nc.vector.quantize_mx(
                        out=live["codes", c][:, a, batch].bitcast(FP8X4),
                        scales=live["scales", c][:, a, batch],
                        in_=live["grouped", c][:, a, batch, :].rearrange("p r t -> p (r t)"),
                    )
            elif c > 0 and r == CHUNK - 1:
                nc.vector.quantize_mx(
                    out=live["codes", c][:].rearrange("p a r -> p (a r)").bitcast(FP8X4),
                    scales=live["scales", c][:].rearrange("p a r -> p (a r)"),
                    in_=live["grouped", c][:].rearrange("p a r t -> p (a r t)"),
                )

        def multiply_z(i):
            c, r = divmod(i, CHUNK)
            batch = slice(r * P, (r + 1) * P)
            acc_z = bank([P, H], F32, "acc_z")
            for a, name in enumerate(("x", "h")):
                nc.tensor.matmul_mx(
                    out=acc_z[:],
                    lhsT=live["codes", c][:, a, batch].bitcast(FP8X4),
                    lhsT_scale=live["scales", c][:, a, batch],
                    rhs=words[name][:, 0 : 2 * H].bitcast(FP4X4),
                    rhs_scale=planes[name][:, 0:H],
                    start=(a == 0),
                    stop=(a == 1),
                )
            live["acc_z", i] = acc_z

        def add_bias_z(i):
            pre_z = work.tile([P, H], F32, bufs=3)
            nc.vector.tensor_tensor(out=pre_z[:], in0=live["acc_z", i][:], in1=bias_z[:], op=ADD)
            live["pre_z", i] = pre_z

        def tanh_z(i):
            c, r = divmod(i, CHUNK)
            if r == 0:
                z_st = stores.tile([P, CHUNK, H], F32, bufs=3)
                live["z", c] = z_st
            nc.scalar.activation(out=live["z", c][:, r, :], in_=live["pre_z", i][:], func=ACT.Tanh)
            n = PAIR if c >= CHUNKS - FINE_STORES else CHUNK
            if (r + 1) % n == 0:
                nc.sync.dma_start(out=z_v[:, i + 1 - n : i + 1, :], in_=live["z", c][:, r + 1 - n : r + 1, :])

        def multiply_m(b):
            c, j = divmod(b, BLOCKS)
            acc_t = bank([P, ROWS], F32, "acc_t")
            for a, name in enumerate(("x", "h")):
                nc.tensor.matmul_mx(
                    out=acc_t[:],
                    lhsT=words[name][:, 2 * (H + j * P) : 2 * (H + (j + 1) * P)].bitcast(FP4X4),
                    lhsT_scale=planes[name][:, H + j * P : H + (j + 1) * P],
                    rhs=live["codes", c][:, a, :].bitcast(FP8X4),
                    rhs_scale=live["scales", c][:, a, :],
                    start=(a == 0),
                    stop=(a == 1),
                )
            live["acc_t", b] = acc_t

        def tanh_m(b):
            j = b % BLOCKS
            tanh_t = work.tile([P, ROWS], F32, bufs=3)
            nc.scalar.activation(
                out=tanh_t[:], in_=live["acc_t", b][:], func=ACT.Tanh, bias=sums[:, BLOCKS + j : BLOCKS + j + 1]
            )
            live["tanh_t", b] = tanh_t

        def turn_back(b):
            back = bank([P, CHUNK, P], F32, "back")
            for r in range(CHUNK):
                nc.tensor.transpose(back[:, r, :], live["tanh_t", b][:, r * P : (r + 1) * P], ident[:])
            live["back", b] = back

        def store_blocks(view, held, c, j):
            n = BLOCKS // 2 if c >= CHUNKS - FINE_STORES else BLOCKS
            if (j + 1) % n == 0:
                cols = slice((j + 1 - n) * P, (j + 1) * P)
                nc.sync.dma_start(out=view[:, c * CHUNK : (c + 1) * CHUNK, cols], in_=held[:, :, cols])

        def scale_m(b):
            c, j = divmod(b, BLOCKS)
            if j == 0:
                m_st = stores.tile([P, CHUNK, H], F32)
                live["m", c] = m_st
            nc.scalar.mul(live["m", c][:, :, j * P : (j + 1) * P], live["back", b][:], M_SCALE)
            store_blocks(m_v, live["m", c], c, j)

        def damp_cell(i):
            c, r = divmod(i, CHUNK)
            if r == 0:
                damped = work.tile([P, CHUNK, H], F32)
                live["damped", c] = damped
            tile, at = part("c", i)
            if r == GPSIMD_DAMPS:
                nc.gpsimd.tensor_tensor(out=live["damped", c][:, r, :], in0=tile[:, at, :], in1=decay_sb[:], op=MULT)
            elif r == 0 or r > GPSIMD_DAMPS:
                n = GPSIMD_DAMPS if r == 0 else 1
                nc.vector.tensor_tensor(
                    out=live["damped", c][:, r : r + n, :],
                    in0=tile[:, at : at + n, :],
                    in1=decay[:].unsqueeze(1).to_broadcast([P, n, H]),
                    op=MULT,
                )

        def product(b):
            c, j = divmod(b, BLOCKS)
            if j == 0:
                i_st = stores.tile([P, CHUNK, H], F32, bufs=3)
                live["i", c] = i_st
            cols = slice(j * P, (j + 1) * P)
            nc.vector.scalar_tensor_tensor(
                out=live["i", c][:, :, cols],
                in0=live["back", b][:],
                scalar=M_SCALE,
                in1=live["damped", c][:, :, cols],
                op0=MULT,
                op1=MULT,
            )

        def total(b):
            c, j = divmod(b, BLOCKS)
            cols = slice(j * P, (j + 1) * P)
            adder = nc.vector if b >= TILES - VECTOR_SUMS else nc.gpsimd
            adder.tensor_tensor(
                out=live["i", c][:, :, cols], in0=live["i", c][:, :, cols], in1=live["z", c][:, :, cols], op=ADD
            )

        def store_total(b):
            c, j = divmod(b, BLOCKS)
            store_blocks(i_v, live["i", c], c, j)

        def run(stage, i):
            if 0 <= i < TILES:
                stage(i)

        for s in range(STEPS):
            run(transpose_tile, s)
            run(scale_m, s - M_OUT)
            run(product, s - PRODUCT)
            run(turn_back, s - TURN_BACK)
            if s == SET_UP:
                set_up()
            run(multiply_m, s - M_MULTIPLY)
            run(multiply_z, s - Z_MULTIPLY)
            run(tanh_m, s - M_TANH)
            run(add_bias_z, s - Z_BIAS)
            run(tanh_z, s - Z_TANH)
            run(damp_cell, s - DAMP)
            if s == SPREAD:
                spread_vectors()
            run(regroup_tile, s)
            run(total, s - TOTAL)
            run(quantise, s - QUANTISE)
            run(store_total, s - TOTAL)
